import numpy as np
import ml_dtypes


def mxq(x, axis, fmt="e4m3"):
    dtype, down = {"e4m3": (ml_dtypes.float8_e4m3fn, 7), "e5m2": (ml_dtypes.float8_e5m2, 14)}[fmt]
    v = np.moveaxis(np.asarray(x, np.float32).astype(ml_dtypes.bfloat16).astype(np.float64), axis, -1)
    blocks = v.reshape(v.shape[:-1] + (-1, 32))
    amax = np.abs(blocks).max(-1, keepdims=True)
    byte = np.maximum(np.where(amax > 0, np.frexp(amax)[1] - 1 + 127, 0) - down, 1)
    scale = np.exp2(byte - 127.0)
    codes = (blocks / scale).astype(np.float32).astype(dtype).astype(np.float64)
    return np.moveaxis((codes * scale).reshape(v.shape), -1, axis)


WIDE = False


def mx_kscale(k):
    if not WIDE:
        return np.ones(k)
    levels = np.array([20, -20, 10, -10, 0])
    a = np.random.permutation(np.resize(levels, k // 512 * 4)).reshape(k // 512, 4)
    idx = np.arange(k)
    return np.exp2(a[idx // 512, idx % 128 // 32])


BF16 = ml_dtypes.bfloat16


def bf(x):
    return np.asarray(x, np.float32).astype(BF16)


def f64(x):
    return np.asarray(x).astype(np.float64)


B, S, HID, NH, NOPE, ROPE, VD, KV_RANK, SW, QB = 1, 1024, 128, 8, 64, 128, 128, 512, 384, 128
QK = NOPE + ROPE


def rotate_half(x):
    h = x.shape[-1] // 2
    return np.concatenate([-x[..., h:], x[..., :h]], axis=-1)


def rotate_half_t(x):
    h = x.shape[-1] // 2
    return np.concatenate([x[..., h:], -x[..., :h]], axis=-1)


def rope_tables():
    pos = np.arange(S, dtype=np.float64)
    inv = 1.0 / (10000.0 ** (np.arange(0, ROPE, 2, dtype=np.float64) / ROPE))
    ang = pos[:, None] * inv[None, :]
    ang = np.concatenate([ang, ang], axis=-1)
    return bf(np.broadcast_to(np.cos(ang)[None], (B, S, ROPE))), bf(np.broadcast_to(np.sin(ang)[None], (B, S, ROPE)))


def setup_inputs():
    s = mx_kscale(S)
    cos, sin = rope_tables()
    hs = np.random.standard_normal((B, S, HID)) * s[None, :, None]
    wq = np.random.standard_normal((HID, NH * QK)) * 2.0 / np.sqrt(HID)
    bq = np.random.standard_normal(NH * QK) * 0.2
    g = np.random.standard_normal((B, NH, S, QK)) * np.exp2(np.random.randint(-12, 1, (B, 1, S, 1))) / s[None, None, :, None]
    return {"hidden_states": bf(hs), "cos": cos, "sin": sin, "Wq": bf(wq), "bq": bf(bq), "grad_out": bf(g)}


def reference(hidden_states, cos, sin, Wq, bq, grad_out):
    g = f64(grad_out)
    c, si = f64(cos)[:, None], f64(sin)[:, None]
    g_nope, g_rope = g[..., :NOPE], g[..., NOPE:]
    d_rope = g_rope * c + rotate_half_t(g_rope * si)
    dq = np.concatenate([g_nope, d_rope], axis=-1).transpose(0, 2, 1, 3).reshape(B * S, NH * QK)
    x = f64(hidden_states).reshape(B * S, HID)
    return mxq(x, 0, "e4m3").T @ mxq(dq, 0, "e5m2")

@@ -1,0 +1,140 @@
+from contextlib import ExitStack
+
+import concourse.mybir as mybir
+
+BF16 = mybir.dt.bfloat16
+F32 = mybir.dt.float32
+U32 = mybir.dt.uint32
+U8 = mybir.dt.uint8
+E4M3_X4 = mybir.dt.float8_e4m3fn_x4
+E5M2_X4 = mybir.dt.float8_e5m2_x4
+MULT = mybir.AluOpType.mult
+ADD = mybir.AluOpType.add
+SUBTRACT = mybir.AluOpType.subtract
+
+P = 128
+PACK = 4
+K_PASS = P * PACK
+TOKENS = 1024
+PASSES = TOKENS // K_PASS
+HID = 128
+HEADS = 8
+NOPE = 64
+ROPE = 128
+HALF = ROPE // 2
+HEAD = NOPE + ROPE
+N_TILE = 512
+GROUP = N_TILE // ROPE
+GROUPS = HEADS // GROUP
+
+FLOPS = 2 * HID * HEADS * HEAD * TOKENS
+BYTES = 2 * (TOKENS * HID + 2 * TOKENS * ROPE + HEADS * TOKENS * HEAD) + 4 * HID * HEADS * HEAD
+
+
+def tile_gptossmlaattention_pb_s_kernel(tc, hidden_states, cos, sin, Wq, bq, grad_out, out):
+    nc = tc.nc
+    with ExitStack() as ctx:
+        keep = ctx.enter_context(tc.tile_pool(name="keep", bufs=1))
+        psum = ctx.enter_context(tc.psum_pool(name="psum", bufs=1))
+
+        cos_sb = keep.tile([P, PASSES, PACK, ROPE], BF16, name="cos_sb")
+        sin_sb = keep.tile([P, PASSES, PACK, ROPE], BF16, name="sin_sb")
+        x_sb = keep.tile([P, PASSES, PACK, HID], BF16, name="x_sb")
+        nc.sync.dma_start(out=cos_sb[:], in_=cos[0].rearrange("(c p j) i -> p c j i", p=P, j=PACK))
+        nc.sync.dma_start(out=sin_sb[:], in_=sin[0].rearrange("(c p j) i -> p c j i", p=P, j=PACK))
+        grads = {}
+        for c in range(PASSES):
+            for g in range(GROUPS):
+                grads[c, g] = keep.tile([P, GROUP, PACK, HEAD], BF16, name="grad_%d_%d" % (c, g))
+                nc.sync.dma_start(
+                    out=grads[c, g][:],
+                    in_=grad_out[0, g * GROUP : (g + 1) * GROUP, c * K_PASS : (c + 1) * K_PASS, :].rearrange(
+                        "h (p j) d -> p h j d", j=PACK
+                    ),
+                )
+                if c == 0 and g == 0:
+                    nc.sync.dma_start(
+                        out=x_sb[:], in_=hidden_states[0].rearrange("(c p j) m -> p c j m", p=P, j=PACK)
+                    )
+
+        x_grouped = keep.tile([P, PASSES, HID, PACK], BF16, name="x_grouped", align_bytes=64)
+        x_codes = keep.tile([P, PASSES, HID], U32, name="x_codes", align_bytes=64)
+        x_scales = keep.tile([P, PASSES, HID], U8, name="x_scales", align_bytes=64)
+        nc.vector.tensor_copy(out=x_grouped[:], in_=x_sb[:].rearrange("p c j m -> p c m j"))
+        nc.vector.quantize_mx(
+            out=x_codes[:].rearrange("p c m -> p (c m)").bitcast(E4M3_X4),
+            scales=x_scales[:].rearrange("p c m -> p (c m)"),
+            in_=x_grouped[:].rearrange("p c m j -> p (c m j)"),
+        )
+
+        acc_nope = psum.tile([P, N_TILE], F32, name="acc_nope")
+        acc_rope = [psum.tile([P, N_TILE], F32, name="acc_rope_%d" % g) for g in range(GROUPS)]
+
+        def multiply(c, acc, codes, scales):
+            nc.tensor.matmul_mx(
+                out=acc[:],
+                lhsT=x_codes[:, c, :].bitcast(E4M3_X4),
+                lhsT_scale=x_scales[:, c, :],
+                rhs=codes[:].bitcast(E5M2_X4),
+                rhs_scale=scales[:],
+                start=(c == 0),
+                stop=(c == PASSES - 1),
+            )
+
+        for c in range(PASSES):
+            nope_grouped = keep.tile([P, HEADS, NOPE, PACK], BF16, name="nope_grouped_%d" % c, align_bytes=64)
+            for g in range(GROUPS):
+                grad = grads[c, g]
+                nc.scalar.copy(
+                    out=nope_grouped[:, g * GROUP : (g + 1) * GROUP],
+                    in_=grad[:, :, :, :NOPE].rearrange("p h j d -> p h d j"),
+                )
+                rotated = grad[:, :, :, NOPE:].rearrange("p h j i -> p h i j")
+                shape = [P, GROUP, ROPE, PACK]
+                by_cos = keep.tile(shape, F32, name="by_cos_%d_%d" % (c, g))
+                by_sin = keep.tile(shape, F32, name="by_sin_%d_%d" % (c, g))
+                nc.vector.tensor_tensor(
+                    out=by_cos[:],
+                    in0=rotated,
+                    in1=cos_sb[:, c].rearrange("p j i -> p i j").unsqueeze(1).to_broadcast(shape),
+                    op=MULT,
+                )
+                nc.vector.tensor_tensor(
+                    out=by_sin[:],
+                    in0=rotated,
+                    in1=sin_sb[:, c].rearrange("p j i -> p i j").unsqueeze(1).to_broadcast(shape),
+                    op=MULT,
+                )
+                rope_grouped = keep.tile(shape, BF16, name="rope_grouped_%d_%d" % (c, g), align_bytes=64)
+                nc.vector.tensor_tensor(
+                    out=rope_grouped[:, :, :HALF], in0=by_cos[:, :, :HALF], in1=by_sin[:, :, HALF:], op=ADD
+                )
+                nc.vector.tensor_tensor(
+                    out=rope_grouped[:, :, HALF:], in0=by_cos[:, :, HALF:], in1=by_sin[:, :, :HALF], op=SUBTRACT
+                )
+                rope_codes = keep.tile([P, N_TILE], U32, name="rope_codes_%d_%d" % (c, g), align_bytes=64)
+                rope_scales = keep.tile([P, N_TILE], U8, name="rope_scales_%d_%d" % (c, g), align_bytes=64)
+                nc.vector.quantize_mx(
+                    out=rope_codes[:].bitcast(E5M2_X4),
+                    scales=rope_scales[:],
+                    in_=rope_grouped[:].rearrange("p h i j -> p (h i j)"),
+                )
+                multiply(c, acc_rope[g], rope_codes, rope_scales)
+            nope_codes = keep.tile([P, N_TILE], U32, name="nope_codes_%d" % c, align_bytes=64)
+            nope_scales = keep.tile([P, N_TILE], U8, name="nope_scales_%d" % c, align_bytes=64)
+            nc.vector.quantize_mx(
+                out=nope_codes[:].bitcast(E5M2_X4),
+                scales=nope_scales[:],
+                in_=nope_grouped[:].rearrange("p h d j -> p (h d j)"),
+            )
+            multiply(c, acc_nope, nope_codes, nope_scales)
+
+        out_sb = keep.tile([P, HEADS, HEAD], F32, name="out_sb")
+        nc.scalar.copy(out=out_sb[:, :, :NOPE], in_=acc_nope[:].rearrange("m (h d) -> m h d", d=NOPE))
+        for g in range(GROUPS):
+            heads = slice(g * GROUP, (g + 1) * GROUP)
+            nc.scalar.copy(out=out_sb[:, heads, NOPE:], in_=acc_rope[g][:].rearrange("m (h i) -> m h i", i=ROPE))
+            nc.sync.dma_start(
+                out=out[:, g * GROUP * HEAD : (g + 1) * GROUP * HEAD],
+                in_=out_sb[:, heads, :].rearrange("m h d -> m (h d)"),
+            )

@@ -1,6 +1,7 @@
 from contextlib import ExitStack
 
 import concourse.mybir as mybir
+from concourse.masks import make_identity
 
 BF16 = mybir.dt.bfloat16
 F32 = mybir.dt.float32
@@ -10,7 +11,6 @@ E4M3_X4 = mybir.dt.float8_e4m3fn_x4
 E5M2_X4 = mybir.dt.float8_e5m2_x4
 MULT = mybir.AluOpType.mult
 ADD = mybir.AluOpType.add
-SUBTRACT = mybir.AluOpType.subtract
 
 P = 128
 PACK = 4
@@ -24,8 +24,13 @@ ROPE = 128
 HALF = ROPE // 2
 HEAD = NOPE + ROPE
 N_TILE = 512
-GROUP = N_TILE // ROPE
-GROUPS = HEADS // GROUP
+CHUNK = 2
+CHUNKS = HEADS // CHUNK
+ROPE_TILES = HEADS * ROPE // N_TILE
+CHUNKS_PER_TILE = CHUNKS // ROPE_TILES
+LAG = 2
+VECTOR_SUMS = 1
+COS, SIN = 0, 1
 
 FLOPS = 2 * HID * HEADS * HEAD * TOKENS
 BYTES = 2 * (TOKENS * HID + 2 * TOKENS * ROPE + HEADS * TOKENS * HEAD) + 4 * HID * HEADS * HEAD
@@ -34,107 +39,164 @@ BYTES = 2 * (TOKENS * HID + 2 * TOKENS * ROPE + HEADS * TOKENS * HEAD) + 4 * HID
 def tile_gptossmlaattention_pb_s_kernel(tc, hidden_states, cos, sin, Wq, bq, grad_out, out):
     nc = tc.nc
     with ExitStack() as ctx:
+        ctx.enter_context(tc.manual_schedule())
         keep = ctx.enter_context(tc.tile_pool(name="keep", bufs=1))
         psum = ctx.enter_context(tc.psum_pool(name="psum", bufs=1))
 
-        cos_sb = keep.tile([P, PASSES, PACK, ROPE], BF16, name="cos_sb")
-        sin_sb = keep.tile([P, PASSES, PACK, ROPE], BF16, name="sin_sb")
+        identity = keep.tile([P, P], BF16, name="identity")
+        make_identity(nc, identity[:])
+
+        steps = [(c, k) for c in range(PASSES) for k in range(CHUNKS)]
+
+        def load_tables(c):
+            tokens = slice(c * K_PASS, (c + 1) * K_PASS)
+            table = keep.tile([P, 2, PACK, ROPE], BF16, name="table_sb_%d" % c)
+            nc.sync.dma_start(out=table[:, COS], in_=cos[0, tokens, :].rearrange("(p j) i -> p j i", j=PACK))
+            nc.sync.dma_start(out=table[:, SIN], in_=sin[0, tokens, :].rearrange("(p j) i -> p j i", j=PACK))
+            return table
+
+        def load_grad(c, k):
+            grad = keep.tile([P, CHUNK, PACK, HEAD], BF16, name="grad_%d_%d" % (c, k))
+            nc.sync.dma_start(
+                out=grad[:],
+                in_=grad_out[0, k * CHUNK : (k + 1) * CHUNK, c * K_PASS : (c + 1) * K_PASS, :].rearrange(
+                    "h (p j) d -> p h j d", j=PACK
+                ),
+            )
+            return grad
+
         x_sb = keep.tile([P, PASSES, PACK, HID], BF16, name="x_sb")
-        nc.sync.dma_start(out=cos_sb[:], in_=cos[0].rearrange("(c p j) i -> p c j i", p=P, j=PACK))
-        nc.sync.dma_start(out=sin_sb[:], in_=sin[0].rearrange("(c p j) i -> p c j i", p=P, j=PACK))
+        table_sb = {}
         grads = {}
-        for c in range(PASSES):
-            for g in range(GROUPS):
-                grads[c, g] = keep.tile([P, GROUP, PACK, HEAD], BF16, name="grad_%d_%d" % (c, g))
-                nc.sync.dma_start(
-                    out=grads[c, g][:],
-                    in_=grad_out[0, g * GROUP : (g + 1) * GROUP, c * K_PASS : (c + 1) * K_PASS, :].rearrange(
-                        "h (p j) d -> p h j d", j=PACK
-                    ),
-                )
-                if c == 0 and g == 0:
-                    nc.sync.dma_start(
-                        out=x_sb[:], in_=hidden_states[0].rearrange("(c p j) m -> p c j m", p=P, j=PACK)
-                    )
+        table_sb[0] = load_tables(0)
+        grads[steps[0]] = load_grad(*steps[0])
+        nc.sync.dma_start(out=x_sb[:], in_=hidden_states[0].rearrange("(c p j) m -> p c j m", p=P, j=PACK))
+        grads[steps[1]] = load_grad(*steps[1])
+        table_sb[1] = load_tables(1)
+        for step in steps[2:]:
+            grads[step] = load_grad(*step)
+
+        table_ps = {}
+
+        def prepare_tables(c):
+            lower_sin = table_sb[c][:, SIN, :, :HALF]
+            nc.vector.tensor_scalar_mul(out=lower_sin, in0=lower_sin, scalar1=-1.0)
+            flipped_ps = psum.tile([P, 2, PACK, P], BF16, name="flipped_ps_%d" % c)
+            for t in (COS, SIN):
+                for j in range(PACK):
+                    nc.tensor.transpose(flipped_ps[:, t, j, :], table_sb[c][:, t, j, :], identity[:])
+            flipped_sb = keep.tile([P, 2, PACK, P], BF16, name="flipped_sb_%d" % c)
+            nc.scalar.copy(out=flipped_sb[:], in_=flipped_ps[:])
+            table_ps[c] = psum.tile([P, 2, PACK, ROPE], BF16, name="table_ps_%d" % c)
+            for t in (COS, SIN):
+                for j in range(PACK):
+                    nc.tensor.transpose(table_ps[c][:, t, j, :], flipped_sb[:, t, j, :], identity[:])
 
         x_grouped = keep.tile([P, PASSES, HID, PACK], BF16, name="x_grouped", align_bytes=64)
         x_codes = keep.tile([P, PASSES, HID], U32, name="x_codes", align_bytes=64)
         x_scales = keep.tile([P, PASSES, HID], U8, name="x_scales", align_bytes=64)
-        nc.vector.tensor_copy(out=x_grouped[:], in_=x_sb[:].rearrange("p c j m -> p c m j"))
-        nc.vector.quantize_mx(
-            out=x_codes[:].rearrange("p c m -> p (c m)").bitcast(E4M3_X4),
-            scales=x_scales[:].rearrange("p c m -> p (c m)"),
-            in_=x_grouped[:].rearrange("p c m j -> p (c m j)"),
-        )
-
+        nope_grouped = {}
+        rope_grouped = {}
+        nope_codes = {}
+        nope_scales = {}
+        rope_codes = {}
+        rope_scales = {}
+        for c in range(PASSES):
+            nope_codes[c] = keep.tile([P, HEADS, NOPE], U32, name="nope_codes_%d" % c, align_bytes=64)
+            nope_scales[c] = keep.tile([P, HEADS, NOPE], U8, name="nope_scales_%d" % c, align_bytes=64)
+            rope_codes[c] = keep.tile([P, HEADS, ROPE], U32, name="rope_codes_%d" % c, align_bytes=64)
+            rope_scales[c] = keep.tile([P, HEADS, ROPE], U8, name="rope_scales_%d" % c, align_bytes=64)
         acc_nope = psum.tile([P, N_TILE], F32, name="acc_nope")
-        acc_rope = [psum.tile([P, N_TILE], F32, name="acc_rope_%d" % g) for g in range(GROUPS)]
+        acc_rope = [psum.tile([P, N_TILE], F32, name="acc_rope_%d" % n) for n in range(ROPE_TILES)]
+
+        def rotate(s):
+            c, k = steps[s]
+            grad = grads[c, k]
+            nope_grouped[s] = keep.tile([P, CHUNK, NOPE, PACK], BF16, name="nope_grouped_%d" % s, align_bytes=64)
+            nc.scalar.copy(out=nope_grouped[s][:], in_=grad[:, :, :, :NOPE].rearrange("p h j d -> p h d j"))
+            table = table_sb[c] if s == 0 else table_ps[c]
+            by_cos = keep.tile([P, CHUNK, ROPE, PACK], F32, name="by_cos_%d" % s)
+            by_sin = keep.tile([P, CHUNK, ROPE, PACK], F32, name="by_sin_%d" % s)
+            nc.vector.tensor_tensor(
+                out=by_cos[:],
+                in0=grad[:, :, :, NOPE:].rearrange("p h j i -> p h i j"),
+                in1=table[:, COS].rearrange("p j i -> p i j").unsqueeze(1).to_broadcast([P, CHUNK, ROPE, PACK]),
+                op=MULT,
+            )
+            for src, dst in ((slice(HALF, ROPE), slice(0, HALF)), (slice(0, HALF), slice(HALF, ROPE))):
+                nc.vector.tensor_tensor(
+                    out=by_sin[:, :, dst, :],
+                    in0=grad[:, :, :, NOPE:][:, :, :, src].rearrange("p h j i -> p h i j"),
+                    in1=table[:, SIN, :, src].rearrange("p j i -> p i j").unsqueeze(1).to_broadcast([P, CHUNK, HALF, PACK]),
+                    op=MULT,
+                )
+            rope_grouped[s] = keep.tile([P, CHUNK, ROPE, PACK], BF16, name="rope_grouped_%d" % s, align_bytes=64)
+            adder = nc.gpsimd if s < len(steps) - VECTOR_SUMS else nc.vector
+            adder.tensor_tensor(out=rope_grouped[s][:], in0=by_cos[:], in1=by_sin[:], op=ADD)
 
         def multiply(c, acc, codes, scales):
             nc.tensor.matmul_mx(
                 out=acc[:],
                 lhsT=x_codes[:, c, :].bitcast(E4M3_X4),
                 lhsT_scale=x_scales[:, c, :],
-                rhs=codes[:].bitcast(E5M2_X4),
-                rhs_scale=scales[:],
+                rhs=codes.bitcast(E5M2_X4),
+                rhs_scale=scales,
                 start=(c == 0),
                 stop=(c == PASSES - 1),
             )
 
-        for c in range(PASSES):
-            nope_grouped = keep.tile([P, HEADS, NOPE, PACK], BF16, name="nope_grouped_%d" % c, align_bytes=64)
-            for g in range(GROUPS):
-                grad = grads[c, g]
-                nc.scalar.copy(
-                    out=nope_grouped[:, g * GROUP : (g + 1) * GROUP],
-                    in_=grad[:, :, :, :NOPE].rearrange("p h j d -> p h d j"),
-                )
-                rotated = grad[:, :, :, NOPE:].rearrange("p h j i -> p h i j")
-                shape = [P, GROUP, ROPE, PACK]
-                by_cos = keep.tile(shape, F32, name="by_cos_%d_%d" % (c, g))
-                by_sin = keep.tile(shape, F32, name="by_sin_%d_%d" % (c, g))
-                nc.vector.tensor_tensor(
-                    out=by_cos[:],
-                    in0=rotated,
-                    in1=cos_sb[:, c].rearrange("p j i -> p i j").unsqueeze(1).to_broadcast(shape),
-                    op=MULT,
-                )
-                nc.vector.tensor_tensor(
-                    out=by_sin[:],
-                    in0=rotated,
-                    in1=sin_sb[:, c].rearrange("p j i -> p i j").unsqueeze(1).to_broadcast(shape),
-                    op=MULT,
-                )
-                rope_grouped = keep.tile(shape, BF16, name="rope_grouped_%d_%d" % (c, g), align_bytes=64)
-                nc.vector.tensor_tensor(
-                    out=rope_grouped[:, :, :HALF], in0=by_cos[:, :, :HALF], in1=by_sin[:, :, HALF:], op=ADD
-                )
-                nc.vector.tensor_tensor(
-                    out=rope_grouped[:, :, HALF:], in0=by_cos[:, :, HALF:], in1=by_sin[:, :, :HALF], op=SUBTRACT
-                )
-                rope_codes = keep.tile([P, N_TILE], U32, name="rope_codes_%d_%d" % (c, g), align_bytes=64)
-                rope_scales = keep.tile([P, N_TILE], U8, name="rope_scales_%d_%d" % (c, g), align_bytes=64)
-                nc.vector.quantize_mx(
-                    out=rope_codes[:].bitcast(E5M2_X4),
-                    scales=rope_scales[:],
-                    in_=rope_grouped[:].rearrange("p h i j -> p (h i j)"),
-                )
-                multiply(c, acc_rope[g], rope_codes, rope_scales)
-            nope_codes = keep.tile([P, N_TILE], U32, name="nope_codes_%d" % c, align_bytes=64)
-            nope_scales = keep.tile([P, N_TILE], U8, name="nope_scales_%d" % c, align_bytes=64)
+        def quantise(s):
+            c, k = steps[s]
+            heads = slice(k * CHUNK, (k + 1) * CHUNK)
             nc.vector.quantize_mx(
-                out=nope_codes[:].bitcast(E5M2_X4),
-                scales=nope_scales[:],
-                in_=nope_grouped[:].rearrange("p h d j -> p (h d j)"),
+                out=nope_codes[c][:, heads].rearrange("p h d -> p (h d)").bitcast(E5M2_X4),
+                scales=nope_scales[c][:, heads].rearrange("p h d -> p (h d)"),
+                in_=nope_grouped[s][:].rearrange("p h d j -> p (h d j)"),
             )
-            multiply(c, acc_nope, nope_codes, nope_scales)
+            nc.vector.quantize_mx(
+                out=rope_codes[c][:, heads].rearrange("p h i -> p (h i)").bitcast(E5M2_X4),
+                scales=rope_scales[c][:, heads].rearrange("p h i -> p (h i)"),
+                in_=rope_grouped[s][:].rearrange("p h i j -> p (h i j)"),
+            )
+            if k == CHUNKS - 1:
+                multiply(
+                    c,
+                    acc_nope,
+                    nope_codes[c][:].rearrange("p h d -> p (h d)"),
+                    nope_scales[c][:].rearrange("p h d -> p (h d)"),
+                )
+            if (k + 1) % CHUNKS_PER_TILE == 0:
+                n = k // CHUNKS_PER_TILE
+                tile_heads = slice(n * CHUNKS_PER_TILE * CHUNK, (n + 1) * CHUNKS_PER_TILE * CHUNK)
+                multiply(
+                    c,
+                    acc_rope[n],
+                    rope_codes[c][:, tile_heads].rearrange("p h i -> p (h i)"),
+                    rope_scales[c][:, tile_heads].rearrange("p h i -> p (h i)"),
+                )
 
-        out_sb = keep.tile([P, HEADS, HEAD], F32, name="out_sb")
-        nc.scalar.copy(out=out_sb[:, :, :NOPE], in_=acc_nope[:].rearrange("m (h d) -> m h d", d=NOPE))
-        for g in range(GROUPS):
-            heads = slice(g * GROUP, (g + 1) * GROUP)
-            nc.scalar.copy(out=out_sb[:, heads, NOPE:], in_=acc_rope[g][:].rearrange("m (h i) -> m h i", i=ROPE))
-            nc.sync.dma_start(
-                out=out[:, g * GROUP * HEAD : (g + 1) * GROUP * HEAD],
-                in_=out_sb[:, heads, :].rearrange("m h d -> m (h d)"),
-            )
+        prepare_tables(0)
+        nc.scalar.copy(out=x_grouped[:], in_=x_sb[:].rearrange("p c j m -> p c m j"))
+        for s in range(LAG):
+            rotate(s)
+        prepare_tables(1)
+        nc.vector.quantize_mx(
+            out=x_codes[:].rearrange("p c m -> p (c m)").bitcast(E4M3_X4),
+            scales=x_scales[:].rearrange("p c m -> p (c m)"),
+            in_=x_grouped[:].rearrange("p c m j -> p (c m j)"),
+        )
+        for s in range(LAG, len(steps)):
+            rotate(s)
+            quantise(s - LAG)
+        for s in range(len(steps) - LAG, len(steps)):
+            quantise(s)
+
+        out_heads = out.rearrange("m (h d) -> m h d", d=HEAD)
+        out_nope = keep.tile([P, HEADS, NOPE], F32, name="out_nope")
+        nc.vector.tensor_copy(out=out_nope[:].rearrange("m h d -> m (h d)"), in_=acc_nope[:])
+        for n in range(ROPE_TILES):
+            tile_heads = slice(n * CHUNKS_PER_TILE * CHUNK, (n + 1) * CHUNKS_PER_TILE * CHUNK)
+            out_rope = keep.tile([P, CHUNKS_PER_TILE * CHUNK, ROPE], F32, name="out_rope_%d" % n)
+            nc.scalar.copy(out=out_rope[:].rearrange("m h i -> m (h i)"), in_=acc_rope[n][:])
+            nc.sync.dma_start(out=out_heads[:, tile_heads, NOPE:], in_=out_rope[:])
+        nc.sync.dma_start(out=out_heads[:, :, :NOPE], in_=out_nope[:])

@@ -24,12 +24,10 @@ ROPE = 128
 HALF = ROPE // 2
 HEAD = NOPE + ROPE
 N_TILE = 512
+TILE_HEADS = N_TILE // ROPE
+ROPE_TILES = HEADS // TILE_HEADS
 CHUNK = 2
-CHUNKS = HEADS // CHUNK
-ROPE_TILES = HEADS * ROPE // N_TILE
-CHUNKS_PER_TILE = CHUNKS // ROPE_TILES
-LAG = 2
-VECTOR_SUMS = 1
+CHUNKS = TILE_HEADS // CHUNK
 COS, SIN = 0, 1
 
 FLOPS = 2 * HID * HEADS * HEAD * TOKENS
@@ -46,7 +44,8 @@ def tile_gptossmlaattention_pb_s_kernel(tc, hidden_states, cos, sin, Wq, bq, gra
         identity = keep.tile([P, P], BF16, name="identity")
         make_identity(nc, identity[:])
 
-        steps = [(c, k) for c in range(PASSES) for k in range(CHUNKS)]
+        operands = [(c, n) for c in range(PASSES) for n in range(ROPE_TILES)]
+        last_chunk = operands[-1] + (CHUNKS - 1,)
 
         def load_tables(c):
             tokens = slice(c * K_PASS, (c + 1) * K_PASS)
@@ -55,26 +54,28 @@ def tile_gptossmlaattention_pb_s_kernel(tc, hidden_states, cos, sin, Wq, bq, gra
             nc.sync.dma_start(out=table[:, SIN], in_=sin[0, tokens, :].rearrange("(p j) i -> p j i", j=PACK))
             return table
 
-        def load_grad(c, k):
-            grad = keep.tile([P, CHUNK, PACK, HEAD], BF16, name="grad_%d_%d" % (c, k))
+        def load_grad(c, n, k):
+            first = n * TILE_HEADS + k * CHUNK
+            grad = keep.tile([P, CHUNK, PACK, HEAD], BF16, name="grad_%d_%d_%d" % (c, n, k))
             nc.sync.dma_start(
                 out=grad[:],
-                in_=grad_out[0, k * CHUNK : (k + 1) * CHUNK, c * K_PASS : (c + 1) * K_PASS, :].rearrange(
+                in_=grad_out[0, first : first + CHUNK, c * K_PASS : (c + 1) * K_PASS, :].rearrange(
                     "h (p j) d -> p h j d", j=PACK
                 ),
             )
             return grad
 
+        chunks = [(c, n, k) for c, n in operands for k in range(CHUNKS)]
         x_sb = keep.tile([P, PASSES, PACK, HID], BF16, name="x_sb")
         table_sb = {}
         grads = {}
         table_sb[0] = load_tables(0)
-        grads[steps[0]] = load_grad(*steps[0])
+        grads[chunks[0]] = load_grad(*chunks[0])
         nc.sync.dma_start(out=x_sb[:], in_=hidden_states[0].rearrange("(c p j) m -> p c j m", p=P, j=PACK))
-        grads[steps[1]] = load_grad(*steps[1])
+        grads[chunks[1]] = load_grad(*chunks[1])
         table_sb[1] = load_tables(1)
-        for step in steps[2:]:
-            grads[step] = load_grad(*step)
+        for chunk in chunks[2:]:
+            grads[chunk] = load_grad(*chunk)
 
         table_ps = {}
 
@@ -95,108 +96,106 @@ def tile_gptossmlaattention_pb_s_kernel(tc, hidden_states, cos, sin, Wq, bq, gra
         x_grouped = keep.tile([P, PASSES, HID, PACK], BF16, name="x_grouped", align_bytes=64)
         x_codes = keep.tile([P, PASSES, HID], U32, name="x_codes", align_bytes=64)
         x_scales = keep.tile([P, PASSES, HID], U8, name="x_scales", align_bytes=64)
-        nope_grouped = {}
+
+        def regroup_x():
+            nc.scalar.copy(out=x_grouped[:], in_=x_sb[:].rearrange("p c j m -> p c m j"))
+
+        def quantise_x():
+            nc.vector.quantize_mx(
+                out=x_codes[:].rearrange("p c m -> p (c m)").bitcast(E4M3_X4),
+                scales=x_scales[:].rearrange("p c m -> p (c m)"),
+                in_=x_grouped[:].rearrange("p c m j -> p (c m j)"),
+            )
+
+        nope_grouped = [
+            keep.tile([P, HEADS, NOPE, PACK], BF16, name="nope_grouped_%d" % c, align_bytes=64) for c in range(PASSES)
+        ]
         rope_grouped = {}
-        nope_codes = {}
-        nope_scales = {}
-        rope_codes = {}
-        rope_scales = {}
-        for c in range(PASSES):
-            nope_codes[c] = keep.tile([P, HEADS, NOPE], U32, name="nope_codes_%d" % c, align_bytes=64)
-            nope_scales[c] = keep.tile([P, HEADS, NOPE], U8, name="nope_scales_%d" % c, align_bytes=64)
-            rope_codes[c] = keep.tile([P, HEADS, ROPE], U32, name="rope_codes_%d" % c, align_bytes=64)
-            rope_scales[c] = keep.tile([P, HEADS, ROPE], U8, name="rope_scales_%d" % c, align_bytes=64)
+
+        def rotate(c, n):
+            rope_grouped[c, n] = keep.tile(
+                [P, TILE_HEADS, ROPE, PACK], BF16, name="rope_grouped_%d_%d" % (c, n), align_bytes=64
+            )
+            for k in range(CHUNKS):
+                grad = grads[c, n, k]
+                first = n * TILE_HEADS + k * CHUNK
+                nc.scalar.copy(
+                    out=nope_grouped[c][:, first : first + CHUNK],
+                    in_=grad[:, :, :, :NOPE].rearrange("p h j d -> p h d j"),
+                )
+                table = table_sb[c] if (c, n, k) == chunks[0] else table_ps[c]
+                rotated = grad[:, :, :, NOPE:]
+                by_cos = keep.tile([P, CHUNK, ROPE, PACK], F32, name="by_cos_%d_%d_%d" % (c, n, k))
+                by_sin = keep.tile([P, CHUNK, ROPE, PACK], F32, name="by_sin_%d_%d_%d" % (c, n, k))
+                nc.vector.tensor_tensor(
+                    out=by_cos[:],
+                    in0=rotated.rearrange("p h j i -> p h i j"),
+                    in1=table[:, COS].rearrange("p j i -> p i j").unsqueeze(1).to_broadcast([P, CHUNK, ROPE, PACK]),
+                    op=MULT,
+                )
+                lower, upper = slice(0, HALF), slice(HALF, ROPE)
+                for src, dst in ((upper, lower), (lower, upper)):
+                    nc.vector.tensor_tensor(
+                        out=by_sin[:, :, dst, :],
+                        in0=rotated[:, :, :, src].rearrange("p h j i -> p h i j"),
+                        in1=table[:, SIN, :, src]
+                        .rearrange("p j i -> p i j")
+                        .unsqueeze(1)
+                        .to_broadcast([P, CHUNK, HALF, PACK]),
+                        op=MULT,
+                    )
+                adder = nc.vector if (c, n, k) == last_chunk else nc.gpsimd
+                adder.tensor_tensor(
+                    out=rope_grouped[c, n][:, k * CHUNK : (k + 1) * CHUNK], in0=by_cos[:], in1=by_sin[:], op=ADD
+                )
+
+        out_heads = out.rearrange("m (h d) -> m h d", d=HEAD)
         acc_nope = psum.tile([P, N_TILE], F32, name="acc_nope")
         acc_rope = [psum.tile([P, N_TILE], F32, name="acc_rope_%d" % n) for n in range(ROPE_TILES)]
 
-        def rotate(s):
-            c, k = steps[s]
-            grad = grads[c, k]
-            nope_grouped[s] = keep.tile([P, CHUNK, NOPE, PACK], BF16, name="nope_grouped_%d" % s, align_bytes=64)
-            nc.scalar.copy(out=nope_grouped[s][:], in_=grad[:, :, :, :NOPE].rearrange("p h j d -> p h d j"))
-            table = table_sb[c] if s == 0 else table_ps[c]
-            by_cos = keep.tile([P, CHUNK, ROPE, PACK], F32, name="by_cos_%d" % s)
-            by_sin = keep.tile([P, CHUNK, ROPE, PACK], F32, name="by_sin_%d" % s)
-            nc.vector.tensor_tensor(
-                out=by_cos[:],
-                in0=grad[:, :, :, NOPE:].rearrange("p h j i -> p h i j"),
-                in1=table[:, COS].rearrange("p j i -> p i j").unsqueeze(1).to_broadcast([P, CHUNK, ROPE, PACK]),
-                op=MULT,
-            )
-            for src, dst in ((slice(HALF, ROPE), slice(0, HALF)), (slice(0, HALF), slice(HALF, ROPE))):
-                nc.vector.tensor_tensor(
-                    out=by_sin[:, :, dst, :],
-                    in0=grad[:, :, :, NOPE:][:, :, :, src].rearrange("p h j i -> p h i j"),
-                    in1=table[:, SIN, :, src].rearrange("p j i -> p i j").unsqueeze(1).to_broadcast([P, CHUNK, HALF, PACK]),
-                    op=MULT,
-                )
-            rope_grouped[s] = keep.tile([P, CHUNK, ROPE, PACK], BF16, name="rope_grouped_%d" % s, align_bytes=64)
-            adder = nc.gpsimd if s < len(steps) - VECTOR_SUMS else nc.vector
-            adder.tensor_tensor(out=rope_grouped[s][:], in0=by_cos[:], in1=by_sin[:], op=ADD)
-
-        def multiply(c, acc, codes, scales):
+        def quantise_and_multiply(c, grouped, acc, out_columns, name):
+            codes = keep.tile([P, N_TILE], U32, name="codes_" + name, align_bytes=64)
+            scales = keep.tile([P, N_TILE], U8, name="scales_" + name, align_bytes=64)
+            nc.vector.quantize_mx(out=codes[:].bitcast(E5M2_X4), scales=scales[:], in_=grouped)
             nc.tensor.matmul_mx(
                 out=acc[:],
                 lhsT=x_codes[:, c, :].bitcast(E4M3_X4),
                 lhsT_scale=x_scales[:, c, :],
-                rhs=codes.bitcast(E5M2_X4),
-                rhs_scale=scales,
+                rhs=codes[:].bitcast(E5M2_X4),
+                rhs_scale=scales[:],
                 start=(c == 0),
                 stop=(c == PASSES - 1),
             )
+            if c == PASSES - 1:
+                result = keep.tile([P, N_TILE], F32, name="result_" + name)
+                nc.scalar.copy(out=result[:], in_=acc[:])
+                nc.sync.dma_start(
+                    out=out_columns, in_=result[:].rearrange("m (h d) -> m h d", h=out_columns.shape[1])
+                )
 
-        def quantise(s):
-            c, k = steps[s]
-            heads = slice(k * CHUNK, (k + 1) * CHUNK)
-            nc.vector.quantize_mx(
-                out=nope_codes[c][:, heads].rearrange("p h d -> p (h d)").bitcast(E5M2_X4),
-                scales=nope_scales[c][:, heads].rearrange("p h d -> p (h d)"),
-                in_=nope_grouped[s][:].rearrange("p h d j -> p (h d j)"),
-            )
-            nc.vector.quantize_mx(
-                out=rope_codes[c][:, heads].rearrange("p h i -> p (h i)").bitcast(E5M2_X4),
-                scales=rope_scales[c][:, heads].rearrange("p h i -> p (h i)"),
-                in_=rope_grouped[s][:].rearrange("p h i j -> p (h i j)"),
-            )
-            if k == CHUNKS - 1:
-                multiply(
+        def finish(c, n):
+            if n == ROPE_TILES - 1:
+                quantise_and_multiply(
                     c,
+                    nope_grouped[c][:].rearrange("p h d j -> p (h d j)"),
                     acc_nope,
-                    nope_codes[c][:].rearrange("p h d -> p (h d)"),
-                    nope_scales[c][:].rearrange("p h d -> p (h d)"),
+                    out_heads[:, :, :NOPE],
+                    "nope_%d" % c,
                 )
-            if (k + 1) % CHUNKS_PER_TILE == 0:
-                n = k // CHUNKS_PER_TILE
-                tile_heads = slice(n * CHUNKS_PER_TILE * CHUNK, (n + 1) * CHUNKS_PER_TILE * CHUNK)
-                multiply(
-                    c,
-                    acc_rope[n],
-                    rope_codes[c][:, tile_heads].rearrange("p h i -> p (h i)"),
-                    rope_scales[c][:, tile_heads].rearrange("p h i -> p (h i)"),
-                )
+            quantise_and_multiply(
+                c,
+                rope_grouped[c, n][:].rearrange("p h i j -> p (h i j)"),
+                acc_rope[n],
+                out_heads[:, n * TILE_HEADS : (n + 1) * TILE_HEADS, NOPE:],
+                "rope_%d_%d" % (c, n),
+            )
 
         prepare_tables(0)
-        nc.scalar.copy(out=x_grouped[:], in_=x_sb[:].rearrange("p c j m -> p c m j"))
-        for s in range(LAG):
-            rotate(s)
+        regroup_x()
+        rotate(*operands[0])
         prepare_tables(1)
-        nc.vector.quantize_mx(
-            out=x_codes[:].rearrange("p c m -> p (c m)").bitcast(E4M3_X4),
-            scales=x_scales[:].rearrange("p c m -> p (c m)"),
-            in_=x_grouped[:].rearrange("p c m j -> p (c m j)"),
-        )
-        for s in range(LAG, len(steps)):
-            rotate(s)
-            quantise(s - LAG)
-        for s in range(len(steps) - LAG, len(steps)):
-            quantise(s)
-
-        out_heads = out.rearrange("m (h d) -> m h d", d=HEAD)
-        out_nope = keep.tile([P, HEADS, NOPE], F32, name="out_nope")
-        nc.vector.tensor_copy(out=out_nope[:].rearrange("m h d -> m (h d)"), in_=acc_nope[:])
-        for n in range(ROPE_TILES):
-            tile_heads = slice(n * CHUNKS_PER_TILE * CHUNK, (n + 1) * CHUNKS_PER_TILE * CHUNK)
-            out_rope = keep.tile([P, CHUNKS_PER_TILE * CHUNK, ROPE], F32, name="out_rope_%d" % n)
-            nc.scalar.copy(out=out_rope[:].rearrange("m h i -> m (h i)"), in_=acc_rope[n][:])
-            nc.sync.dma_start(out=out_heads[:, tile_heads, NOPE:], in_=out_rope[:])
-        nc.sync.dma_start(out=out_heads[:, :, :NOPE], in_=out_nope[:])
+        quantise_x()
+        for t in range(1, len(operands)):
+            rotate(*operands[t])
+            finish(*operands[t - 1])
+        finish(*operands[-1])

@@ -25,9 +25,6 @@ HALF = ROPE // 2
 HEAD = NOPE + ROPE
 N_TILE = 512
 TILE_HEADS = N_TILE // ROPE
-ROPE_TILES = HEADS // TILE_HEADS
-CHUNK = 2
-CHUNKS = TILE_HEADS // CHUNK
 COS, SIN = 0, 1
 
 FLOPS = 2 * HID * HEADS * HEAD * TOKENS
@@ -39,59 +36,67 @@ def tile_gptossmlaattention_pb_s_kernel(tc, hidden_states, cos, sin, Wq, bq, gra
     with ExitStack() as ctx:
         ctx.enter_context(tc.manual_schedule())
         keep = ctx.enter_context(tc.tile_pool(name="keep", bufs=1))
-        psum = ctx.enter_context(tc.psum_pool(name="psum", bufs=1))
+        acc_pool = ctx.enter_context(tc.psum_pool(name="acc", bufs=1))
+        rt_pool = ctx.enter_context(tc.psum_pool(name="rt", bufs=3))
+        sum_pool = ctx.enter_context(tc.psum_pool(name="sum", bufs=2))
 
-        identity = keep.tile([P, P], BF16, name="identity")
-        make_identity(nc, identity[:])
+        table_sb = [keep.tile([P, 2, PACK, ROPE], BF16, name="table_sb_%d" % c) for c in range(PASSES)]
 
-        operands = [(c, n) for c in range(PASSES) for n in range(ROPE_TILES)]
-        last_chunk = operands[-1] + (CHUNKS - 1,)
-
-        def load_tables(c):
-            tokens = slice(c * K_PASS, (c + 1) * K_PASS)
-            table = keep.tile([P, 2, PACK, ROPE], BF16, name="table_sb_%d" % c)
-            nc.sync.dma_start(out=table[:, COS], in_=cos[0, tokens, :].rearrange("(p j) i -> p j i", j=PACK))
-            nc.sync.dma_start(out=table[:, SIN], in_=sin[0, tokens, :].rearrange("(p j) i -> p j i", j=PACK))
-            return table
-
-        def load_grad(c, n, k):
-            first = n * TILE_HEADS + k * CHUNK
-            grad = keep.tile([P, CHUNK, PACK, HEAD], BF16, name="grad_%d_%d_%d" % (c, n, k))
+        def load_table(c, t):
             nc.sync.dma_start(
-                out=grad[:],
-                in_=grad_out[0, first : first + CHUNK, c * K_PASS : (c + 1) * K_PASS, :].rearrange(
+                out=table_sb[c][:, t],
+                in_=(cos, sin)[t][0, c * K_PASS : (c + 1) * K_PASS, :].rearrange("(p j) i -> p j i", j=PACK),
+            )
+
+        grad = {}
+        groups = {}
+
+        def load_grad(c, first, count):
+            loaded = keep.tile([P, count, PACK, HEAD], BF16, name="grad_%d_%d" % (c, first))
+            nc.sync.dma_start(
+                out=loaded[:],
+                in_=grad_out[0, first : first + count, c * K_PASS : (c + 1) * K_PASS, :].rearrange(
                     "h (p j) d -> p h j d", j=PACK
                 ),
             )
-            return grad
+            groups[c, first] = loaded
+            for h in range(count):
+                grad[c, first + h] = loaded[:, h]
 
-        chunks = [(c, n, k) for c, n in operands for k in range(CHUNKS)]
         x_sb = keep.tile([P, PASSES, PACK, HID], BF16, name="x_sb")
-        table_sb = {}
-        grads = {}
-        table_sb[0] = load_tables(0)
-        grads[chunks[0]] = load_grad(*chunks[0])
+        load_table(0, COS)
+        load_table(0, SIN)
+        load_grad(0, 4, 2)
+        load_grad(0, 0, 1)
+        load_grad(0, 1, 1)
+        load_table(1, SIN)
+        load_table(1, COS)
+        load_grad(0, 2, 2)
+        load_grad(0, 6, 2)
         nc.sync.dma_start(out=x_sb[:], in_=hidden_states[0].rearrange("(c p j) m -> p c j m", p=P, j=PACK))
-        grads[chunks[1]] = load_grad(*chunks[1])
-        table_sb[1] = load_tables(1)
-        for chunk in chunks[2:]:
-            grads[chunk] = load_grad(*chunk)
+        for first in range(0, HEADS, 2):
+            load_grad(1, first, 2)
 
-        table_ps = {}
+        ident_bf = keep.tile([P, P], BF16, name="ident_bf")
+        make_identity(nc, ident_bf[:])
+        ident_f = keep.tile([P, P], F32, name="ident_f")
+        swap_f = keep.tile([P, P], F32, name="swap_f")
+        nc.vector.tensor_copy(out=ident_f[:], in_=ident_bf[:])
+        nc.vector.tensor_copy(out=swap_f[:, :HALF], in_=ident_bf[:, HALF:])
+        nc.vector.tensor_copy(out=swap_f[:, HALF:], in_=ident_bf[:, :HALF])
 
-        def prepare_tables(c):
+        table_t = [keep.tile([P, 2, PACK, P], BF16, name="table_t_%d" % c) for c in range(PASSES)]
+
+        def negate_lower_sin(c):
             lower_sin = table_sb[c][:, SIN, :, :HALF]
             nc.vector.tensor_scalar_mul(out=lower_sin, in0=lower_sin, scalar1=-1.0)
-            flipped_ps = psum.tile([P, 2, PACK, P], BF16, name="flipped_ps_%d" % c)
-            for t in (COS, SIN):
+
+        def flip_table(c, kinds):
+            flipped = rt_pool.tile([P, len(kinds), PACK, P], BF16, name="rt")
+            for place, t in enumerate(kinds):
                 for j in range(PACK):
-                    nc.tensor.transpose(flipped_ps[:, t, j, :], table_sb[c][:, t, j, :], identity[:])
-            flipped_sb = keep.tile([P, 2, PACK, P], BF16, name="flipped_sb_%d" % c)
-            nc.scalar.copy(out=flipped_sb[:], in_=flipped_ps[:])
-            table_ps[c] = psum.tile([P, 2, PACK, ROPE], BF16, name="table_ps_%d" % c)
-            for t in (COS, SIN):
-                for j in range(PACK):
-                    nc.tensor.transpose(table_ps[c][:, t, j, :], flipped_sb[:, t, j, :], identity[:])
+                    nc.tensor.transpose(flipped[:, place, j, :], table_sb[c][:, t, j, :], ident_bf[:])
+            return flipped
 
         x_grouped = keep.tile([P, PASSES, HID, PACK], BF16, name="x_grouped", align_bytes=64)
         x_codes = keep.tile([P, PASSES, HID], U32, name="x_codes", align_bytes=64)
@@ -110,48 +115,102 @@ def tile_gptossmlaattention_pb_s_kernel(tc, hidden_states, cos, sin, Wq, bq, gra
         nope_grouped = [
             keep.tile([P, HEADS, NOPE, PACK], BF16, name="nope_grouped_%d" % c, align_bytes=64) for c in range(PASSES)
         ]
-        rope_grouped = {}
+        rope_grouped = {
+            (c, n): keep.tile([P, TILE_HEADS, ROPE, PACK], BF16, name="rope_grouped_%d_%d" % (c, n), align_bytes=64)
+            for c in range(PASSES)
+            for n in range(HEADS // TILE_HEADS)
+        }
 
-        def rotate(c, n):
-            rope_grouped[c, n] = keep.tile(
-                [P, TILE_HEADS, ROPE, PACK], BF16, name="rope_grouped_%d_%d" % (c, n), align_bytes=64
+        def regroup_nope(c, first):
+            loaded = groups[c, first][:]
+            nc.scalar.copy(
+                out=nope_grouped[c][:, first : first + loaded.shape[1]],
+                in_=loaded[:, :, :, :NOPE].rearrange("p h j d -> p h d j"),
             )
-            for k in range(CHUNKS):
-                grad = grads[c, n, k]
-                first = n * TILE_HEADS + k * CHUNK
-                nc.scalar.copy(
-                    out=nope_grouped[c][:, first : first + CHUNK],
-                    in_=grad[:, :, :, :NOPE].rearrange("p h j d -> p h d j"),
+
+        r_t = {}
+        prod_t = {}
+        sums = {}
+
+        def transpose_r(c, h):
+            r_t[c, h] = rt_pool.tile([P, PACK, P], BF16, name="rt")
+            for j in range(PACK):
+                nc.tensor.transpose(r_t[c, h][:, j, :], grad[c, h][:, j, NOPE:], ident_bf[:])
+
+        def products(c, h):
+            prod_t[c, h] = keep.tile([P, 2, PACK, P], F32, name="prod_t_%d_%d" % (c, h))
+            nc.vector.tensor_tensor(
+                out=prod_t[c, h][:],
+                in0=r_t[c, h][:].unsqueeze(1).to_broadcast([P, 2, PACK, P]),
+                in1=table_t[c][:],
+                op=MULT,
+            )
+
+        def add_up(c, h):
+            sums[c, h] = sum_pool.tile([P, PACK, ROPE], F32, name="sum")
+            for j in range(PACK):
+                nc.tensor.matmul(
+                    out=sums[c, h][:, j, :],
+                    lhsT=prod_t[c, h][:, COS, j, :],
+                    rhs=ident_f[:],
+                    is_transpose=True,
+                    start=True,
+                    stop=False,
                 )
-                table = table_sb[c] if (c, n, k) == chunks[0] else table_ps[c]
-                rotated = grad[:, :, :, NOPE:]
-                by_cos = keep.tile([P, CHUNK, ROPE, PACK], F32, name="by_cos_%d_%d_%d" % (c, n, k))
-                by_sin = keep.tile([P, CHUNK, ROPE, PACK], F32, name="by_sin_%d_%d_%d" % (c, n, k))
-                nc.vector.tensor_tensor(
-                    out=by_cos[:],
-                    in0=rotated.rearrange("p h j i -> p h i j"),
-                    in1=table[:, COS].rearrange("p j i -> p i j").unsqueeze(1).to_broadcast([P, CHUNK, ROPE, PACK]),
+                nc.tensor.matmul(
+                    out=sums[c, h][:, j, :],
+                    lhsT=prod_t[c, h][:, SIN, j, :],
+                    rhs=swap_f[:],
+                    is_transpose=True,
+                    start=False,
+                    stop=True,
+                )
+
+        def round_out(c, h):
+            nc.scalar.copy(
+                out=rope_grouped[c, h // TILE_HEADS][:, h % TILE_HEADS],
+                in_=sums[c, h][:].rearrange("p j i -> p i j"),
+            )
+
+        natural = {}
+
+        def natural_cos(engine, c, first):
+            by_cos = keep.tile([P, 2, ROPE, PACK], F32, name="by_cos_%d_%d" % (c, first))
+            natural[c, first, COS] = by_cos
+            engine.tensor_tensor(
+                out=by_cos[:],
+                in0=groups[c, first][:, :, :, NOPE:].rearrange("p h j i -> p h i j"),
+                in1=table_sb[c][:, COS].rearrange("p j i -> p i j").unsqueeze(1).to_broadcast([P, 2, ROPE, PACK]),
+                op=MULT,
+            )
+
+        def natural_sin(engine, c, first):
+            by_sin = keep.tile([P, 2, ROPE, PACK], F32, name="by_sin_%d_%d" % (c, first))
+            natural[c, first, SIN] = by_sin
+            lower, upper = slice(0, HALF), slice(HALF, ROPE)
+            for src, dst in ((upper, lower), (lower, upper)):
+                engine.tensor_tensor(
+                    out=by_sin[:, :, dst, :],
+                    in0=groups[c, first][:, :, :, NOPE:][:, :, :, src].rearrange("p h j i -> p h i j"),
+                    in1=table_sb[c][:, SIN, :, src]
+                    .rearrange("p j i -> p i j")
+                    .unsqueeze(1)
+                    .to_broadcast([P, 2, HALF, PACK]),
                     op=MULT,
                 )
-                lower, upper = slice(0, HALF), slice(HALF, ROPE)
-                for src, dst in ((upper, lower), (lower, upper)):
-                    nc.vector.tensor_tensor(
-                        out=by_sin[:, :, dst, :],
-                        in0=rotated[:, :, :, src].rearrange("p h j i -> p h i j"),
-                        in1=table[:, SIN, :, src]
-                        .rearrange("p j i -> p i j")
-                        .unsqueeze(1)
-                        .to_broadcast([P, CHUNK, HALF, PACK]),
-                        op=MULT,
-                    )
-                adder = nc.vector if (c, n, k) == last_chunk else nc.gpsimd
-                adder.tensor_tensor(
-                    out=rope_grouped[c, n][:, k * CHUNK : (k + 1) * CHUNK], in0=by_cos[:], in1=by_sin[:], op=ADD
-                )
+
+        def natural_add(engine, c, first):
+            place = first % TILE_HEADS
+            engine.tensor_tensor(
+                out=rope_grouped[c, first // TILE_HEADS][:, place : place + 2],
+                in0=natural[c, first, COS][:],
+                in1=natural[c, first, SIN][:],
+                op=ADD,
+            )
 
         out_heads = out.rearrange("m (h d) -> m h d", d=HEAD)
-        acc_nope = psum.tile([P, N_TILE], F32, name="acc_nope")
-        acc_rope = [psum.tile([P, N_TILE], F32, name="acc_rope_%d" % n) for n in range(ROPE_TILES)]
+        acc_nope = acc_pool.tile([P, N_TILE], F32, name="acc_nope")
+        acc_rope = [acc_pool.tile([P, N_TILE], F32, name="acc_rope_%d" % n) for n in range(HEADS // TILE_HEADS)]
 
         def quantise_and_multiply(c, grouped, acc, out_columns, name):
             codes = keep.tile([P, N_TILE], U32, name="codes_" + name, align_bytes=64)
@@ -173,15 +232,7 @@ def tile_gptossmlaattention_pb_s_kernel(tc, hidden_states, cos, sin, Wq, bq, gra
                     out=out_columns, in_=result[:].rearrange("m (h d) -> m h d", h=out_columns.shape[1])
                 )
 
-        def finish(c, n):
-            if n == ROPE_TILES - 1:
-                quantise_and_multiply(
-                    c,
-                    nope_grouped[c][:].rearrange("p h d j -> p (h d j)"),
-                    acc_nope,
-                    out_heads[:, :, :NOPE],
-                    "nope_%d" % c,
-                )
+        def finish_rope(c, n):
             quantise_and_multiply(
                 c,
                 rope_grouped[c, n][:].rearrange("p h i j -> p (h i j)"),
@@ -190,12 +241,63 @@ def tile_gptossmlaattention_pb_s_kernel(tc, hidden_states, cos, sin, Wq, bq, gra
                 "rope_%d_%d" % (c, n),
             )
 
-        prepare_tables(0)
-        regroup_x()
-        rotate(*operands[0])
-        prepare_tables(1)
-        quantise_x()
-        for t in range(1, len(operands)):
-            rotate(*operands[t])
-            finish(*operands[t - 1])
-        finish(*operands[-1])
+        def finish_nope(c):
+            quantise_and_multiply(
+                c, nope_grouped[c][:].rearrange("p h d j -> p (h d j)"), acc_nope, out_heads[:, :, :NOPE], "nope_%d" % c
+            )
+
+        units = [(0, h) for h in range(TILE_HEADS)] + [(1, h) for h in range(HEADS)]
+
+        flipped_cos = flip_table(0, (COS,))
+        negate_lower_sin(0)
+        flipped_sin = flip_table(0, (SIN,))
+        transpose_r(*units[0])
+        nc.scalar.copy(out=table_t[0][:, COS], in_=flipped_cos[:, 0])
+        nc.scalar.copy(out=table_t[0][:, SIN], in_=flipped_sin[:, 0])
+        transpose_r(*units[1])
+        transpose_r(*units[2])
+        natural_cos(nc.vector, 0, 4)
+        natural_sin(nc.gpsimd, 0, 4)
+        natural_add(nc.gpsimd, 0, 4)
+        natural_cos(nc.gpsimd, 0, 6)
+        natural_sin(nc.gpsimd, 0, 6)
+        natural_add(nc.gpsimd, 0, 6)
+
+        next_flip = {0: units[3], 1: "tables"}
+        for t in range(2, len(units) - 2):
+            next_flip[t] = units[t + 2]
+        scalar_extra = {
+            0: lambda: regroup_nope(0, 0),
+            1: lambda: regroup_nope(0, 1),
+            2: regroup_x,
+            3: lambda: regroup_nope(0, 2),
+            4: lambda: regroup_nope(0, 4),
+            5: lambda: regroup_nope(0, 6),
+            6: lambda: regroup_nope(1, 0),
+            7: lambda: regroup_nope(1, 2),
+            8: lambda: regroup_nope(1, 4),
+            9: lambda: regroup_nope(1, 6),
+        }
+        vector_extra = {
+            0: lambda: negate_lower_sin(1),
+            3: quantise_x,
+            5: lambda: finish_rope(0, 0),
+            7: lambda: finish_nope(0),
+            9: lambda: finish_rope(1, 0),
+            11: lambda: (finish_rope(0, 1), finish_nope(1)),
+        }
+        for t, unit in enumerate(units):
+            products(*unit)
+            add_up(*unit)
+            flip = next_flip.get(t)
+            if flip == "tables":
+                flipped = flip_table(1, (COS, SIN))
+                nc.scalar.copy(out=table_t[1][:], in_=flipped[:])
+            elif flip is not None:
+                transpose_r(*flip)
+            round_out(*unit)
+            if t in vector_extra:
+                vector_extra[t]()
+            if t in scalar_extra:
+                scalar_extra[t]()
+        finish_rope(1, 1)

@@ -11,6 +11,7 @@ E4M3_X4 = mybir.dt.float8_e4m3fn_x4
 E5M2_X4 = mybir.dt.float8_e5m2_x4
 MULT = mybir.AluOpType.mult
 ADD = mybir.AluOpType.add
+COPY = mybir.ActivationFunctionType.Copy
 
 P = 128
 PACK = 4
@@ -36,8 +37,8 @@ def tile_gptossmlaattention_pb_s_kernel(tc, hidden_states, cos, sin, Wq, bq, gra
     with ExitStack() as ctx:
         ctx.enter_context(tc.manual_schedule())
         keep = ctx.enter_context(tc.tile_pool(name="keep", bufs=1))
-        acc_pool = ctx.enter_context(tc.psum_pool(name="acc", bufs=1))
-        rt_pool = ctx.enter_context(tc.psum_pool(name="rt", bufs=3))
+        fixed = ctx.enter_context(tc.psum_pool(name="fixed", bufs=1))
+        rt_pool = ctx.enter_context(tc.psum_pool(name="rt", bufs=2))
         sum_pool = ctx.enter_context(tc.psum_pool(name="sum", bufs=2))
 
         table_sb = [keep.tile([P, 2, PACK, ROPE], BF16, name="table_sb_%d" % c) for c in range(PASSES)]
@@ -66,37 +67,42 @@ def tile_gptossmlaattention_pb_s_kernel(tc, hidden_states, cos, sin, Wq, bq, gra
         x_sb = keep.tile([P, PASSES, PACK, HID], BF16, name="x_sb")
         load_table(0, COS)
         load_table(0, SIN)
-        load_grad(0, 4, 2)
-        load_grad(0, 0, 1)
-        load_grad(0, 1, 1)
+        load_grad(0, 0, 2)
         load_table(1, SIN)
         load_table(1, COS)
-        load_grad(0, 2, 2)
         load_grad(0, 6, 2)
+        load_grad(1, 0, 1)
+        load_grad(0, 2, 2)
+        load_grad(1, 1, 1)
+        load_grad(1, 2, 2)
+        load_grad(0, 4, 2)
         nc.sync.dma_start(out=x_sb[:], in_=hidden_states[0].rearrange("(c p j) m -> p c j m", p=P, j=PACK))
-        for first in range(0, HEADS, 2):
-            load_grad(1, first, 2)
+        load_grad(1, 4, 2)
+        load_grad(1, 6, 2)
 
         ident_bf = keep.tile([P, P], BF16, name="ident_bf")
         make_identity(nc, ident_bf[:])
+        sign = keep.tile([P, 1], F32, name="sign")
+        nc.gpsimd.memset(sign[:], 1.0)
+        nc.gpsimd.memset(sign[:HALF], -1.0)
         ident_f = keep.tile([P, P], F32, name="ident_f")
         swap_f = keep.tile([P, P], F32, name="swap_f")
         nc.vector.tensor_copy(out=ident_f[:], in_=ident_bf[:])
         nc.vector.tensor_copy(out=swap_f[:, :HALF], in_=ident_bf[:, HALF:])
         nc.vector.tensor_copy(out=swap_f[:, HALF:], in_=ident_bf[:, :HALF])
 
-        table_t = [keep.tile([P, 2, PACK, P], BF16, name="table_t_%d" % c) for c in range(PASSES)]
+        table_ps = fixed.tile([P, 2, PACK, ROPE], BF16, name="table_ps")
 
-        def negate_lower_sin(c):
-            lower_sin = table_sb[c][:, SIN, :, :HALF]
-            nc.vector.tensor_scalar_mul(out=lower_sin, in0=lower_sin, scalar1=-1.0)
+        def copy_table_to_psum(t):
+            nc.tensor.matmul(
+                out=table_ps[:, t].rearrange("p j i -> p (j i)"),
+                lhsT=ident_bf[:],
+                rhs=table_sb[0][:, t].rearrange("p j i -> p (j i)"),
+                start=True,
+                stop=True,
+            )
 
-        def flip_table(c, kinds):
-            flipped = rt_pool.tile([P, len(kinds), PACK, P], BF16, name="rt")
-            for place, t in enumerate(kinds):
-                for j in range(PACK):
-                    nc.tensor.transpose(flipped[:, place, j, :], table_sb[c][:, t, j, :], ident_bf[:])
-            return flipped
+        table_t = keep.tile([P, 2, PACK, P], BF16, name="table_t")
 
         x_grouped = keep.tile([P, PASSES, HID, PACK], BF16, name="x_grouped", align_bytes=64)
         x_codes = keep.tile([P, PASSES, HID], U32, name="x_codes", align_bytes=64)
@@ -132,87 +138,88 @@ def tile_gptossmlaattention_pb_s_kernel(tc, hidden_states, cos, sin, Wq, bq, gra
         prod_t = {}
         sums = {}
 
-        def transpose_r(c, h):
-            r_t[c, h] = rt_pool.tile([P, PACK, P], BF16, name="rt")
+        def transpose_r(h):
+            r_t[h] = rt_pool.tile([P, PACK, P], BF16, name="rt")
             for j in range(PACK):
-                nc.tensor.transpose(r_t[c, h][:, j, :], grad[c, h][:, j, NOPE:], ident_bf[:])
+                nc.tensor.transpose(r_t[h][:, j, :], grad[1, h][:, j, NOPE:], ident_bf[:])
 
-        def products(c, h):
-            prod_t[c, h] = keep.tile([P, 2, PACK, P], F32, name="prod_t_%d_%d" % (c, h))
+        def products(h):
+            prod_t[h] = keep.tile([P, 2, PACK, P], F32, name="prod_t_%d" % h)
             nc.vector.tensor_tensor(
-                out=prod_t[c, h][:],
-                in0=r_t[c, h][:].unsqueeze(1).to_broadcast([P, 2, PACK, P]),
-                in1=table_t[c][:],
+                out=prod_t[h][:],
+                in0=r_t[h][:].unsqueeze(1).to_broadcast([P, 2, PACK, P]),
+                in1=table_t[:],
                 op=MULT,
             )
 
-        def add_up(c, h):
-            sums[c, h] = sum_pool.tile([P, PACK, ROPE], F32, name="sum")
+        def add_up(h):
+            sums[h] = sum_pool.tile([P, PACK, ROPE], F32, name="sum")
             for j in range(PACK):
                 nc.tensor.matmul(
-                    out=sums[c, h][:, j, :],
-                    lhsT=prod_t[c, h][:, COS, j, :],
-                    rhs=ident_f[:],
-                    is_transpose=True,
-                    start=True,
-                    stop=False,
+                    out=sums[h][:, j, :], lhsT=prod_t[h][:, COS, j, :], rhs=ident_f[:],
+                    is_transpose=True, start=True, stop=False,
                 )
                 nc.tensor.matmul(
-                    out=sums[c, h][:, j, :],
-                    lhsT=prod_t[c, h][:, SIN, j, :],
-                    rhs=swap_f[:],
-                    is_transpose=True,
-                    start=False,
-                    stop=True,
+                    out=sums[h][:, j, :], lhsT=prod_t[h][:, SIN, j, :], rhs=swap_f[:],
+                    is_transpose=True, start=False, stop=True,
                 )
 
-        def round_out(c, h):
+        def round_out(h):
             nc.scalar.copy(
-                out=rope_grouped[c, h // TILE_HEADS][:, h % TILE_HEADS],
-                in_=sums[c, h][:].rearrange("p j i -> p i j"),
+                out=rope_grouped[1, h // TILE_HEADS][:, h % TILE_HEADS],
+                in_=sums[h][:].rearrange("p j i -> p i j"),
             )
 
         natural = {}
 
-        def natural_cos(engine, c, first):
-            by_cos = keep.tile([P, 2, ROPE, PACK], F32, name="by_cos_%d_%d" % (c, first))
-            natural[c, first, COS] = by_cos
+        on_vector = (nc.vector, table_ps)
+        on_gpsimd = (nc.gpsimd, table_sb[0])
+
+        def natural_cos(worker, first):
+            engine, table = worker
+            by_cos = keep.tile([P, 2, ROPE, PACK], F32, name="by_cos_%d" % first)
+            natural[first, COS] = by_cos
             engine.tensor_tensor(
                 out=by_cos[:],
-                in0=groups[c, first][:, :, :, NOPE:].rearrange("p h j i -> p h i j"),
-                in1=table_sb[c][:, COS].rearrange("p j i -> p i j").unsqueeze(1).to_broadcast([P, 2, ROPE, PACK]),
+                in0=groups[0, first][:, :, :, NOPE:].rearrange("p h j i -> p h i j"),
+                in1=table[:, COS]
+                .rearrange("p j i -> p i j")
+                .unsqueeze(1)
+                .to_broadcast([P, 2, ROPE, PACK]),
                 op=MULT,
             )
 
-        def natural_sin(engine, c, first):
-            by_sin = keep.tile([P, 2, ROPE, PACK], F32, name="by_sin_%d_%d" % (c, first))
-            natural[c, first, SIN] = by_sin
+        def natural_sin(worker, first):
+            engine, table = worker
+            by_sin = keep.tile([P, 2, ROPE, PACK], F32, name="by_sin_%d" % first)
+            natural[first, SIN] = by_sin
             lower, upper = slice(0, HALF), slice(HALF, ROPE)
             for src, dst in ((upper, lower), (lower, upper)):
                 engine.tensor_tensor(
                     out=by_sin[:, :, dst, :],
-                    in0=groups[c, first][:, :, :, NOPE:][:, :, :, src].rearrange("p h j i -> p h i j"),
-                    in1=table_sb[c][:, SIN, :, src]
+                    in0=groups[0, first][:, :, :, NOPE:][:, :, :, src].rearrange("p h j i -> p h i j"),
+                    in1=table[:, SIN, :, src]
                     .rearrange("p j i -> p i j")
                     .unsqueeze(1)
                     .to_broadcast([P, 2, HALF, PACK]),
                     op=MULT,
                 )
 
-        def natural_add(engine, c, first):
+        def natural_add(worker, first):
+            engine, table = worker
             place = first % TILE_HEADS
             engine.tensor_tensor(
-                out=rope_grouped[c, first // TILE_HEADS][:, place : place + 2],
-                in0=natural[c, first, COS][:],
-                in1=natural[c, first, SIN][:],
+                out=rope_grouped[0, first // TILE_HEADS][:, place : place + 2],
+                in0=natural[first, COS][:],
+                in1=natural[first, SIN][:],
                 op=ADD,
             )
 
         out_heads = out.rearrange("m (h d) -> m h d", d=HEAD)
-        acc_nope = acc_pool.tile([P, N_TILE], F32, name="acc_nope")
-        acc_rope = [acc_pool.tile([P, N_TILE], F32, name="acc_rope_%d" % n) for n in range(HEADS // TILE_HEADS)]
+        acc_nope = fixed.tile([P, N_TILE], F32, name="acc_nope")
+        acc_rope = [fixed.tile([P, N_TILE], F32, name="acc_rope_%d" % n) for n in range(HEADS // TILE_HEADS)]
 
-        def quantise_and_multiply(c, grouped, acc, out_columns, name):
+        def quantise_and_multiply(c, grouped, acc, out_columns, name, first_pass):
             codes = keep.tile([P, N_TILE], U32, name="codes_" + name, align_bytes=64)
             scales = keep.tile([P, N_TILE], U8, name="scales_" + name, align_bytes=64)
             nc.vector.quantize_mx(out=codes[:].bitcast(E5M2_X4), scales=scales[:], in_=grouped)
@@ -222,82 +229,81 @@ def tile_gptossmlaattention_pb_s_kernel(tc, hidden_states, cos, sin, Wq, bq, gra
                 lhsT_scale=x_scales[:, c, :],
                 rhs=codes[:].bitcast(E5M2_X4),
                 rhs_scale=scales[:],
-                start=(c == 0),
-                stop=(c == PASSES - 1),
+                start=first_pass,
+                stop=not first_pass,
             )
-            if c == PASSES - 1:
+            if not first_pass:
                 result = keep.tile([P, N_TILE], F32, name="result_" + name)
                 nc.scalar.copy(out=result[:], in_=acc[:])
                 nc.sync.dma_start(
                     out=out_columns, in_=result[:].rearrange("m (h d) -> m h d", h=out_columns.shape[1])
                 )
 
-        def finish_rope(c, n):
+        def finish_rope(c, n, first_pass):
             quantise_and_multiply(
                 c,
                 rope_grouped[c, n][:].rearrange("p h i j -> p (h i j)"),
                 acc_rope[n],
                 out_heads[:, n * TILE_HEADS : (n + 1) * TILE_HEADS, NOPE:],
                 "rope_%d_%d" % (c, n),
+                first_pass,
             )
 
-        def finish_nope(c):
+        def finish_nope(c, first_pass):
             quantise_and_multiply(
-                c, nope_grouped[c][:].rearrange("p h d j -> p (h d j)"), acc_nope, out_heads[:, :, :NOPE], "nope_%d" % c
+                c,
+                nope_grouped[c][:].rearrange("p h d j -> p (h d j)"),
+                acc_nope,
+                out_heads[:, :, :NOPE],
+                "nope_%d" % c,
+                first_pass,
             )
 
-        units = [(0, h) for h in range(TILE_HEADS)] + [(1, h) for h in range(HEADS)]
+        copy_table_to_psum(COS)
+        lower_sin = table_sb[0][:, SIN, :, :HALF]
+        nc.vector.tensor_scalar_mul(out=lower_sin, in0=lower_sin, scalar1=-1.0)
+        copy_table_to_psum(SIN)
+        flipped = rt_pool.tile([P, 2, PACK, P], BF16, name="rt")
+        for t in (SIN, COS):
+            for j in range(PACK):
+                nc.tensor.transpose(flipped[:, t, j, :], table_sb[1][:, t, j, :], ident_bf[:])
+        transpose_r(0)
+        regroup_nope(0, 0)
+        nc.scalar.activation(out=table_t[:, SIN], in_=flipped[:, SIN], func=COPY, scale=sign[:, 0:1])
+        nc.scalar.copy(out=table_t[:, COS], in_=flipped[:, COS])
+        transpose_r(1)
+        regroup_nope(0, 6)
+        natural_cos(on_vector, 0)
+        natural_sin(on_vector, 0)
+        natural_cos(on_gpsimd, 6)
+        natural_sin(on_gpsimd, 6)
+        natural_add(on_gpsimd, 6)
+        natural_add(on_gpsimd, 0)
 
-        flipped_cos = flip_table(0, (COS,))
-        negate_lower_sin(0)
-        flipped_sin = flip_table(0, (SIN,))
-        transpose_r(*units[0])
-        nc.scalar.copy(out=table_t[0][:, COS], in_=flipped_cos[:, 0])
-        nc.scalar.copy(out=table_t[0][:, SIN], in_=flipped_sin[:, 0])
-        transpose_r(*units[1])
-        transpose_r(*units[2])
-        natural_cos(nc.vector, 0, 4)
-        natural_sin(nc.gpsimd, 0, 4)
-        natural_add(nc.gpsimd, 0, 4)
-        natural_cos(nc.gpsimd, 0, 6)
-        natural_sin(nc.gpsimd, 0, 6)
-        natural_add(nc.gpsimd, 0, 6)
-
-        next_flip = {0: units[3], 1: "tables"}
-        for t in range(2, len(units) - 2):
-            next_flip[t] = units[t + 2]
-        scalar_extra = {
-            0: lambda: regroup_nope(0, 0),
-            1: lambda: regroup_nope(0, 1),
-            2: regroup_x,
-            3: lambda: regroup_nope(0, 2),
-            4: lambda: regroup_nope(0, 4),
-            5: lambda: regroup_nope(0, 6),
-            6: lambda: regroup_nope(1, 0),
-            7: lambda: regroup_nope(1, 2),
-            8: lambda: regroup_nope(1, 4),
-            9: lambda: regroup_nope(1, 6),
-        }
         vector_extra = {
-            0: lambda: negate_lower_sin(1),
-            3: quantise_x,
-            5: lambda: finish_rope(0, 0),
-            7: lambda: finish_nope(0),
-            9: lambda: finish_rope(1, 0),
-            11: lambda: (finish_rope(0, 1), finish_nope(1)),
+            0: lambda: natural_cos(on_vector, 2),
+            1: lambda: (natural_sin(on_vector, 2), natural_add(on_gpsimd, 2)),
+            2: lambda: (natural_cos(on_vector, 4), natural_sin(on_gpsimd, 4), natural_add(on_gpsimd, 4)),
+            3: lambda: (quantise_x(), finish_nope(0, True)),
+            4: lambda: finish_rope(1, 0, True),
+            5: lambda: finish_nope(1, False),
+            7: lambda: (finish_rope(0, 0, False), finish_rope(0, 1, True)),
         }
-        for t, unit in enumerate(units):
-            products(*unit)
-            add_up(*unit)
-            flip = next_flip.get(t)
-            if flip == "tables":
-                flipped = flip_table(1, (COS, SIN))
-                nc.scalar.copy(out=table_t[1][:], in_=flipped[:])
-            elif flip is not None:
-                transpose_r(*flip)
-            round_out(*unit)
-            if t in vector_extra:
-                vector_extra[t]()
-            if t in scalar_extra:
-                scalar_extra[t]()
-        finish_rope(1, 1)
+        scalar_extra = {
+            0: lambda: regroup_nope(0, 2),
+            1: lambda: (regroup_nope(0, 4), regroup_x()),
+            2: lambda: (regroup_nope(1, 0), regroup_nope(1, 1)),
+            3: lambda: (regroup_nope(1, 2), regroup_nope(1, 4)),
+            4: lambda: regroup_nope(1, 6),
+        }
+        for h in range(HEADS):
+            products(h)
+            if h + 2 < HEADS:
+                transpose_r(h + 2)
+            add_up(h)
+            round_out(h)
+            if h in vector_extra:
+                vector_extra[h]()
+            if h in scalar_extra:
+                scalar_extra[h]()
+        finish_rope(1, 1, False)

@@ -147,8 +147,8 @@ def tile_gptossmlaattention_pb_s_kernel(tc, hidden_states, cos, sin, Wq, bq, gra
             prod_t[h] = keep.tile([P, 2, PACK, P], F32, name="prod_t_%d" % h)
             nc.vector.tensor_tensor(
                 out=prod_t[h][:],
-                in0=r_t[h][:].unsqueeze(1).to_broadcast([P, 2, PACK, P]),
-                in1=table_t[:],
+                in0=table_t[:],
+                in1=r_t[h][:].unsqueeze(1).to_broadcast([P, 2, PACK, P]),
                 op=MULT,
             )
 

@@ -11,7 +11,6 @@ E4M3_X4 = mybir.dt.float8_e4m3fn_x4
 E5M2_X4 = mybir.dt.float8_e5m2_x4
 MULT = mybir.AluOpType.mult
 ADD = mybir.AluOpType.add
-COPY = mybir.ActivationFunctionType.Copy
 
 P = 128
 PACK = 4
@@ -27,6 +26,7 @@ HEAD = NOPE + ROPE
 N_TILE = 512
 TILE_HEADS = N_TILE // ROPE
 COS, SIN = 0, 1
+ROAD_HEADS = 6
 
 FLOPS = 2 * HID * HEADS * HEAD * TOKENS
 BYTES = 2 * (TOKENS * HID + 2 * TOKENS * ROPE + HEADS * TOKENS * HEAD) + 4 * HID * HEADS * HEAD
@@ -70,21 +70,18 @@ def tile_gptossmlaattention_pb_s_kernel(tc, hidden_states, cos, sin, Wq, bq, gra
         load_grad(0, 0, 2)
         load_table(1, SIN)
         load_table(1, COS)
-        load_grad(0, 6, 2)
         load_grad(1, 0, 1)
-        load_grad(0, 2, 2)
+        load_grad(1, 6, 2)
         load_grad(1, 1, 1)
+        load_grad(0, 2, 2)
         load_grad(1, 2, 2)
         load_grad(0, 4, 2)
         nc.sync.dma_start(out=x_sb[:], in_=hidden_states[0].rearrange("(c p j) m -> p c j m", p=P, j=PACK))
         load_grad(1, 4, 2)
-        load_grad(1, 6, 2)
+        load_grad(0, 6, 2)
 
         ident_bf = keep.tile([P, P], BF16, name="ident_bf")
         make_identity(nc, ident_bf[:])
-        sign = keep.tile([P, 1], F32, name="sign")
-        nc.gpsimd.memset(sign[:], 1.0)
-        nc.gpsimd.memset(sign[:HALF], -1.0)
         ident_f = keep.tile([P, P], F32, name="ident_f")
         swap_f = keep.tile([P, P], F32, name="swap_f")
         nc.vector.tensor_copy(out=ident_f[:], in_=ident_bf[:])
@@ -171,48 +168,45 @@ def tile_gptossmlaattention_pb_s_kernel(tc, hidden_states, cos, sin, Wq, bq, gra
             )
 
         natural = {}
+        on_vector = (nc.vector, (table_ps, None))
+        on_gpsimd = (nc.gpsimd, table_sb)
 
-        on_vector = (nc.vector, table_ps)
-        on_gpsimd = (nc.gpsimd, table_sb[0])
-
-        def natural_cos(worker, first):
-            engine, table = worker
-            by_cos = keep.tile([P, 2, ROPE, PACK], F32, name="by_cos_%d" % first)
-            natural[first, COS] = by_cos
+        def natural_cos(worker, c, first):
+            engine, tables = worker
+            by_cos = keep.tile([P, 2, PACK, ROPE], F32, name="by_cos_%d_%d" % (c, first))
+            natural[c, first, COS] = by_cos
             engine.tensor_tensor(
                 out=by_cos[:],
-                in0=groups[0, first][:, :, :, NOPE:].rearrange("p h j i -> p h i j"),
-                in1=table[:, COS]
-                .rearrange("p j i -> p i j")
-                .unsqueeze(1)
-                .to_broadcast([P, 2, ROPE, PACK]),
+                in0=groups[c, first][:, :, :, NOPE:],
+                in1=tables[c][:, COS].unsqueeze(1).to_broadcast([P, 2, PACK, ROPE]),
                 op=MULT,
             )
 
-        def natural_sin(worker, first):
-            engine, table = worker
-            by_sin = keep.tile([P, 2, ROPE, PACK], F32, name="by_sin_%d" % first)
-            natural[first, SIN] = by_sin
+        def natural_sin(worker, c, first):
+            engine, tables = worker
+            by_sin = keep.tile([P, 2, PACK, ROPE], F32, name="by_sin_%d_%d" % (c, first))
+            natural[c, first, SIN] = by_sin
             lower, upper = slice(0, HALF), slice(HALF, ROPE)
             for src, dst in ((upper, lower), (lower, upper)):
                 engine.tensor_tensor(
-                    out=by_sin[:, :, dst, :],
-                    in0=groups[0, first][:, :, :, NOPE:][:, :, :, src].rearrange("p h j i -> p h i j"),
-                    in1=table[:, SIN, :, src]
-                    .rearrange("p j i -> p i j")
-                    .unsqueeze(1)
-                    .to_broadcast([P, 2, HALF, PACK]),
+                    out=by_sin[:, :, :, dst],
+                    in0=groups[c, first][:, :, :, NOPE:][:, :, :, src],
+                    in1=tables[c][:, SIN, :, src].unsqueeze(1).to_broadcast([P, 2, PACK, HALF]),
                     op=MULT,
                 )
 
-        def natural_add(worker, first):
-            engine, table = worker
+        def natural_add(c, first):
+            summed = keep.tile([P, 2, PACK, ROPE], BF16, name="summed_%d_%d" % (c, first))
+            natural[c, first, "sum"] = summed
+            nc.gpsimd.tensor_tensor(
+                out=summed[:], in0=natural[c, first, COS][:], in1=natural[c, first, SIN][:], op=ADD
+            )
+
+        def interleave(c, first):
             place = first % TILE_HEADS
-            engine.tensor_tensor(
-                out=rope_grouped[0, first // TILE_HEADS][:, place : place + 2],
-                in0=natural[first, COS][:],
-                in1=natural[first, SIN][:],
-                op=ADD,
+            nc.scalar.copy(
+                out=rope_grouped[c, first // TILE_HEADS][:, place : place + 2],
+                in_=natural[c, first, "sum"][:].rearrange("p h j i -> p h i j"),
             )
 
         out_heads = out.rearrange("m (h d) -> m h d", d=HEAD)
@@ -259,51 +253,69 @@ def tile_gptossmlaattention_pb_s_kernel(tc, hidden_states, cos, sin, Wq, bq, gra
                 first_pass,
             )
 
+        def negate_lower_sin(c):
+            lower_sin = table_sb[c][:, SIN, :, :HALF]
+            nc.vector.tensor_scalar_mul(out=lower_sin, in0=lower_sin, scalar1=-1.0)
+
+        def unit(h):
+            products(h)
+            if h + 2 < ROAD_HEADS:
+                transpose_r(h + 2)
+            add_up(h)
+            round_out(h)
+
         copy_table_to_psum(COS)
-        lower_sin = table_sb[0][:, SIN, :, :HALF]
-        nc.vector.tensor_scalar_mul(out=lower_sin, in0=lower_sin, scalar1=-1.0)
+        negate_lower_sin(0)
         copy_table_to_psum(SIN)
+        negate_lower_sin(1)
         flipped = rt_pool.tile([P, 2, PACK, P], BF16, name="rt")
         for t in (SIN, COS):
             for j in range(PACK):
                 nc.tensor.transpose(flipped[:, t, j, :], table_sb[1][:, t, j, :], ident_bf[:])
         transpose_r(0)
         regroup_nope(0, 0)
-        nc.scalar.activation(out=table_t[:, SIN], in_=flipped[:, SIN], func=COPY, scale=sign[:, 0:1])
-        nc.scalar.copy(out=table_t[:, COS], in_=flipped[:, COS])
+        nc.scalar.copy(out=table_t[:], in_=flipped[:])
         transpose_r(1)
-        regroup_nope(0, 6)
-        natural_cos(on_vector, 0)
-        natural_sin(on_vector, 0)
-        natural_cos(on_gpsimd, 6)
-        natural_sin(on_gpsimd, 6)
-        natural_add(on_gpsimd, 6)
-        natural_add(on_gpsimd, 0)
 
-        vector_extra = {
-            0: lambda: natural_cos(on_vector, 2),
-            1: lambda: (natural_sin(on_vector, 2), natural_add(on_gpsimd, 2)),
-            2: lambda: (natural_cos(on_vector, 4), natural_sin(on_gpsimd, 4), natural_add(on_gpsimd, 4)),
-            3: lambda: (quantise_x(), finish_nope(0, True)),
-            4: lambda: finish_rope(1, 0, True),
-            5: lambda: finish_nope(1, False),
-            7: lambda: (finish_rope(0, 0, False), finish_rope(0, 1, True)),
-        }
-        scalar_extra = {
-            0: lambda: regroup_nope(0, 2),
-            1: lambda: (regroup_nope(0, 4), regroup_x()),
-            2: lambda: (regroup_nope(1, 0), regroup_nope(1, 1)),
-            3: lambda: (regroup_nope(1, 2), regroup_nope(1, 4)),
-            4: lambda: regroup_nope(1, 6),
-        }
-        for h in range(HEADS):
-            products(h)
-            if h + 2 < HEADS:
-                transpose_r(h + 2)
-            add_up(h)
-            round_out(h)
-            if h in vector_extra:
-                vector_extra[h]()
-            if h in scalar_extra:
-                scalar_extra[h]()
-        finish_rope(1, 1, False)
+        natural_cos(on_vector, 0, 0)
+        natural_sin(on_vector, 0, 0)
+        natural_cos(on_gpsimd, 1, 6)
+        natural_add(0, 0)
+        unit(0)
+        regroup_nope(1, 0)
+        regroup_nope(1, 6)
+        natural_cos(on_vector, 0, 2)
+        unit(1)
+        regroup_nope(1, 1)
+        regroup_nope(0, 2)
+        natural_sin(on_vector, 0, 2)
+        natural_sin(on_gpsimd, 1, 6)
+        natural_add(0, 2)
+        interleave(0, 0)
+        unit(2)
+        regroup_nope(1, 2)
+        natural_cos(on_vector, 0, 4)
+        unit(3)
+        regroup_nope(0, 4)
+        regroup_x()
+        natural_sin(on_vector, 0, 4)
+        natural_add(1, 6)
+        natural_add(0, 4)
+        interleave(0, 2)
+        unit(4)
+        regroup_nope(1, 4)
+        natural_cos(on_vector, 0, 6)
+        unit(5)
+        regroup_nope(0, 6)
+        natural_sin(on_vector, 0, 6)
+        natural_add(0, 6)
+        interleave(1, 6)
+        interleave(0, 4)
+        quantise_x()
+        finish_nope(0, True)
+        finish_nope(1, False)
+        finish_rope(1, 0, True)
+        interleave(0, 6)
+        finish_rope(0, 0, False)
+        finish_rope(1, 1, True)
+        finish_rope(0, 1, False)

@@ -255,7 +255,10 @@ def tile_gptossmlaattention_pb_s_kernel(tc, hidden_states, cos, sin, Wq, bq, gra
 
         def negate_lower_sin(c):
             lower_sin = table_sb[c][:, SIN, :, :HALF]
-            nc.vector.tensor_scalar_mul(out=lower_sin, in0=lower_sin, scalar1=-1.0)
+            if c == 0:
+                nc.vector.tensor_scalar_mul(out=lower_sin, in0=lower_sin, scalar1=-1.0)
+            else:
+                nc.scalar.mul(out=lower_sin, in_=lower_sin, mul=-1.0)
 
         def unit(h):
             products(h)
@@ -281,41 +284,41 @@ def tile_gptossmlaattention_pb_s_kernel(tc, hidden_states, cos, sin, Wq, bq, gra
         natural_sin(on_vector, 0, 0)
         natural_cos(on_gpsimd, 1, 6)
         natural_add(0, 0)
-        unit(0)
         regroup_nope(1, 0)
         regroup_nope(1, 6)
-        natural_cos(on_vector, 0, 2)
-        unit(1)
         regroup_nope(1, 1)
         regroup_nope(0, 2)
+        regroup_nope(1, 2)
+        regroup_nope(0, 4)
+        unit(0)
+        natural_cos(on_vector, 0, 2)
+        interleave(0, 0)
+        unit(1)
+        regroup_x()
+        regroup_nope(1, 4)
         natural_sin(on_vector, 0, 2)
         natural_sin(on_gpsimd, 1, 6)
         natural_add(0, 2)
-        interleave(0, 0)
         unit(2)
-        regroup_nope(1, 2)
+        interleave(0, 2)
         natural_cos(on_vector, 0, 4)
         unit(3)
-        regroup_nope(0, 4)
-        regroup_x()
         natural_sin(on_vector, 0, 4)
         natural_add(1, 6)
         natural_add(0, 4)
-        interleave(0, 2)
+        interleave(1, 6)
         unit(4)
-        regroup_nope(1, 4)
+        interleave(0, 4)
         natural_cos(on_vector, 0, 6)
         unit(5)
         regroup_nope(0, 6)
         natural_sin(on_vector, 0, 6)
         natural_add(0, 6)
-        interleave(1, 6)
-        interleave(0, 4)
-        quantise_x()
-        finish_nope(0, True)
-        finish_nope(1, False)
-        finish_rope(1, 0, True)
         interleave(0, 6)
+        quantise_x()
+        finish_rope(1, 0, True)
         finish_rope(0, 0, False)
+        finish_nope(1, True)
         finish_rope(1, 1, True)
+        finish_nope(0, False)
         finish_rope(0, 1, False)

@@ -195,10 +195,10 @@ def tile_gptossmlaattention_pb_s_kernel(tc, hidden_states, cos, sin, Wq, bq, gra
                     op=MULT,
                 )
 
-        def natural_add(c, first):
+        def natural_add(c, first, engine=nc.gpsimd):
             summed = keep.tile([P, 2, PACK, ROPE], BF16, name="summed_%d_%d" % (c, first))
             natural[c, first, "sum"] = summed
-            nc.gpsimd.tensor_tensor(
+            engine.tensor_tensor(
                 out=summed[:], in0=natural[c, first, COS][:], in1=natural[c, first, SIN][:], op=ADD
             )
 
@@ -313,9 +313,9 @@ def tile_gptossmlaattention_pb_s_kernel(tc, hidden_states, cos, sin, Wq, bq, gra
         unit(5)
         regroup_nope(0, 6)
         natural_sin(on_vector, 0, 6)
-        natural_add(0, 6)
-        interleave(0, 6)
         quantise_x()
+        natural_add(0, 6, nc.vector)
+        interleave(0, 6)
         finish_rope(1, 0, True)
         finish_rope(0, 0, False)
         finish_nope(1, True)

@@ -51,29 +51,37 @@ def tile_gptossmlaattention_pb_s_kernel(tc, hidden_states, cos, sin, Wq, bq, gra
 
         grad = {}
         groups = {}
+        group_of = {}
+        for c, first, count in (
+            (0, 0, 2), (0, 2, 2), (0, 4, 2), (0, 6, 2), (1, 0, 1), (1, 1, 1), (1, 2, 2), (1, 4, 2), (1, 6, 2)
+        ):
+            group = keep.tile([P, count, PACK, HEAD], BF16, name="grad_%d_%d" % (c, first))
+            groups[c, first] = group
+            for h in range(count):
+                grad[c, first + h] = group[:, h]
+                group_of[c, first + h] = first
 
-        def load_grad(c, first, count):
-            loaded = keep.tile([P, count, PACK, HEAD], BF16, name="grad_%d_%d" % (c, first))
+        def load_grad(c, head, count):
+            place = head - group_of[c, head]
             nc.sync.dma_start(
-                out=loaded[:],
-                in_=grad_out[0, first : first + count, c * K_PASS : (c + 1) * K_PASS, :].rearrange(
+                out=groups[c, group_of[c, head]][:, place : place + count],
+                in_=grad_out[0, head : head + count, c * K_PASS : (c + 1) * K_PASS, :].rearrange(
                     "h (p j) d -> p h j d", j=PACK
                 ),
             )
-            groups[c, first] = loaded
-            for h in range(count):
-                grad[c, first + h] = loaded[:, h]
 
         x_sb = keep.tile([P, PASSES, PACK, HID], BF16, name="x_sb")
         load_table(0, COS)
+        load_grad(0, 0, 1)
         load_table(0, SIN)
-        load_grad(0, 0, 2)
-        load_table(1, SIN)
+        load_grad(0, 1, 1)
         load_table(1, COS)
-        load_grad(1, 0, 1)
-        load_grad(1, 6, 2)
-        load_grad(1, 1, 1)
+        load_grad(1, 6, 1)
+        load_table(1, SIN)
         load_grad(0, 2, 2)
+        load_grad(1, 7, 1)
+        load_grad(1, 0, 1)
+        load_grad(1, 1, 1)
         load_grad(1, 2, 2)
         load_grad(0, 4, 2)
         nc.sync.dma_start(out=x_sb[:], in_=hidden_states[0].rearrange("(c p j) m -> p c j m", p=P, j=PACK))
@@ -84,6 +92,8 @@ def tile_gptossmlaattention_pb_s_kernel(tc, hidden_states, cos, sin, Wq, bq, gra
         make_identity(nc, ident_bf[:])
         ident_f = keep.tile([P, P], F32, name="ident_f")
         swap_f = keep.tile([P, P], F32, name="swap_f")
+        minus_ident_bf = keep.tile([P, P], BF16, name="minus_ident_bf")
+        nc.vector.tensor_scalar_mul(out=minus_ident_bf[:], in0=ident_bf[:], scalar1=-1.0)
         nc.vector.tensor_copy(out=ident_f[:], in_=ident_bf[:])
         nc.vector.tensor_copy(out=swap_f[:, :HALF], in_=ident_bf[:, HALF:])
         nc.vector.tensor_copy(out=swap_f[:, HALF:], in_=ident_bf[:, :HALF])
@@ -91,13 +101,23 @@ def tile_gptossmlaattention_pb_s_kernel(tc, hidden_states, cos, sin, Wq, bq, gra
         table_ps = fixed.tile([P, 2, PACK, ROPE], BF16, name="table_ps")
 
         def copy_table_to_psum(t):
-            nc.tensor.matmul(
-                out=table_ps[:, t].rearrange("p j i -> p (j i)"),
-                lhsT=ident_bf[:],
-                rhs=table_sb[0][:, t].rearrange("p j i -> p (j i)"),
-                start=True,
-                stop=True,
-            )
+            if t == COS:
+                nc.tensor.matmul(
+                    out=table_ps[:, t].rearrange("p j i -> p (j i)"),
+                    lhsT=ident_bf[:],
+                    rhs=table_sb[0][:, t].rearrange("p j i -> p (j i)"),
+                    start=True,
+                    stop=True,
+                )
+            else:
+                for half, matrix in ((slice(0, HALF), minus_ident_bf), (slice(HALF, ROPE), ident_bf)):
+                    nc.tensor.matmul(
+                        out=table_ps[:, t, :, half],
+                        lhsT=matrix[:],
+                        rhs=table_sb[0][:, t, :, half],
+                        start=True,
+                        stop=True,
+                    )
 
         table_t = keep.tile([P, 2, PACK, P], BF16, name="table_t")
 
@@ -124,11 +144,11 @@ def tile_gptossmlaattention_pb_s_kernel(tc, hidden_states, cos, sin, Wq, bq, gra
             for n in range(HEADS // TILE_HEADS)
         }
 
-        def regroup_nope(c, first):
-            loaded = groups[c, first][:]
+        def regroup_nope(c, head, count):
+            place = head - group_of[c, head]
             nc.scalar.copy(
-                out=nope_grouped[c][:, first : first + loaded.shape[1]],
-                in_=loaded[:, :, :, :NOPE].rearrange("p h j d -> p h d j"),
+                out=nope_grouped[c][:, head : head + count],
+                in_=groups[c, group_of[c, head]][:, place : place + count, :, :NOPE].rearrange("p h j d -> p h d j"),
             )
 
         r_t = {}
@@ -169,16 +189,18 @@ def tile_gptossmlaattention_pb_s_kernel(tc, hidden_states, cos, sin, Wq, bq, gra
 
         natural = {}
         on_vector = (nc.vector, (table_ps, None))
+        on_vector_from_sbuf = (nc.vector, table_sb)
         on_gpsimd = (nc.gpsimd, table_sb)
 
-        def natural_cos(worker, c, first):
+        def natural_cos(worker, c, first, place=0, count=2):
             engine, tables = worker
-            by_cos = keep.tile([P, 2, PACK, ROPE], F32, name="by_cos_%d_%d" % (c, first))
-            natural[c, first, COS] = by_cos
+            if (c, first, COS) not in natural:
+                by_cos = keep.tile([P, 2, PACK, ROPE], F32, name="by_cos_%d_%d" % (c, first))
+                natural[c, first, COS] = by_cos
             engine.tensor_tensor(
-                out=by_cos[:],
-                in0=groups[c, first][:, :, :, NOPE:],
-                in1=tables[c][:, COS].unsqueeze(1).to_broadcast([P, 2, PACK, ROPE]),
+                out=natural[c, first, COS][:, place : place + count],
+                in0=groups[c, first][:, place : place + count, :, NOPE:],
+                in1=tables[c][:, COS].unsqueeze(1).to_broadcast([P, count, PACK, ROPE]),
                 op=MULT,
             )
 
@@ -255,10 +277,7 @@ def tile_gptossmlaattention_pb_s_kernel(tc, hidden_states, cos, sin, Wq, bq, gra
 
         def negate_lower_sin(c):
             lower_sin = table_sb[c][:, SIN, :, :HALF]
-            if c == 0:
-                nc.vector.tensor_scalar_mul(out=lower_sin, in0=lower_sin, scalar1=-1.0)
-            else:
-                nc.scalar.mul(out=lower_sin, in_=lower_sin, mul=-1.0)
+            nc.scalar.mul(out=lower_sin, in_=lower_sin, mul=-1.0)
 
         def unit(h):
             products(h)
@@ -268,57 +287,59 @@ def tile_gptossmlaattention_pb_s_kernel(tc, hidden_states, cos, sin, Wq, bq, gra
             round_out(h)
 
         copy_table_to_psum(COS)
-        negate_lower_sin(0)
+        natural_cos(on_vector_from_sbuf, 0, 0, 0, 1)
         copy_table_to_psum(SIN)
+        regroup_nope(0, 0, 1)
+        natural_cos(on_vector_from_sbuf, 0, 0, 1, 1)
+        regroup_nope(0, 1, 1)
+        natural_cos(on_gpsimd, 1, 6, 0, 1)
         negate_lower_sin(1)
         flipped = rt_pool.tile([P, 2, PACK, P], BF16, name="rt")
-        for t in (SIN, COS):
+        for t in (COS, SIN):
             for j in range(PACK):
                 nc.tensor.transpose(flipped[:, t, j, :], table_sb[1][:, t, j, :], ident_bf[:])
+        natural_sin(on_vector, 0, 0)
+        natural_cos(on_gpsimd, 1, 6, 1, 1)
         transpose_r(0)
-        regroup_nope(0, 0)
         nc.scalar.copy(out=table_t[:], in_=flipped[:])
         transpose_r(1)
-
-        natural_cos(on_vector, 0, 0)
-        natural_sin(on_vector, 0, 0)
-        natural_cos(on_gpsimd, 1, 6)
         natural_add(0, 0)
-        regroup_nope(1, 0)
-        regroup_nope(1, 6)
-        regroup_nope(1, 1)
-        regroup_nope(0, 2)
-        regroup_nope(1, 2)
-        regroup_nope(0, 4)
-        unit(0)
         natural_cos(on_vector, 0, 2)
+        regroup_nope(1, 6, 1)
+        regroup_nope(0, 2, 2)
+        regroup_nope(1, 7, 1)
+        regroup_nope(1, 0, 1)
+        regroup_nope(1, 1, 1)
+        natural_sin(on_vector, 0, 2)
+        natural_sin(on_gpsimd, 1, 6)
+        regroup_nope(1, 2, 2)
+        regroup_nope(0, 4, 2)
+        unit(0)
+        natural_cos(on_vector, 0, 4)
         interleave(0, 0)
         unit(1)
         regroup_x()
-        regroup_nope(1, 4)
-        natural_sin(on_vector, 0, 2)
-        natural_sin(on_gpsimd, 1, 6)
+        regroup_nope(1, 4, 2)
+        natural_sin(on_vector, 0, 4)
         natural_add(0, 2)
         unit(2)
+        regroup_nope(0, 6, 2)
+        natural_cos(on_vector, 0, 6)
         interleave(0, 2)
-        natural_cos(on_vector, 0, 4)
         unit(3)
-        natural_sin(on_vector, 0, 4)
+        natural_sin(on_vector, 0, 6)
         natural_add(1, 6)
         natural_add(0, 4)
         interleave(1, 6)
         unit(4)
-        interleave(0, 4)
-        natural_cos(on_vector, 0, 6)
         unit(5)
-        regroup_nope(0, 6)
-        natural_sin(on_vector, 0, 6)
+        interleave(0, 4)
         quantise_x()
         natural_add(0, 6, nc.vector)
         interleave(0, 6)
-        finish_rope(1, 0, True)
-        finish_rope(0, 0, False)
         finish_nope(1, True)
-        finish_rope(1, 1, True)
         finish_nope(0, False)
+        finish_rope(0, 0, True)
+        finish_rope(1, 0, False)
+        finish_rope(1, 1, True)
         finish_rope(0, 1, False)

@@ -281,10 +281,9 @@ def tile_gptossmlaattention_pb_s_kernel(tc, hidden_states, cos, sin, Wq, bq, gra
 
         def unit(h):
             products(h)
+            add_up(h)
             if h + 2 < ROAD_HEADS:
                 transpose_r(h + 2)
-            add_up(h)
-            round_out(h)
 
         copy_table_to_psum(COS)
         natural_cos(on_vector_from_sbuf, 0, 0, 0, 1)
@@ -317,29 +316,35 @@ def tile_gptossmlaattention_pb_s_kernel(tc, hidden_states, cos, sin, Wq, bq, gra
         unit(0)
         natural_cos(on_vector, 0, 4)
         interleave(0, 0)
-        unit(1)
         regroup_x()
+        round_out(0)
         regroup_nope(1, 4, 2)
+        unit(1)
+        regroup_nope(0, 6, 2)
+        round_out(1)
         natural_sin(on_vector, 0, 4)
         natural_add(0, 2)
         unit(2)
-        regroup_nope(0, 6, 2)
-        natural_cos(on_vector, 0, 6)
         interleave(0, 2)
+        round_out(2)
+        natural_cos(on_vector, 0, 6)
         unit(3)
         natural_sin(on_vector, 0, 6)
         natural_add(1, 6)
         natural_add(0, 4)
         interleave(1, 6)
+        round_out(3)
         unit(4)
         unit(5)
         interleave(0, 4)
+        round_out(4)
         quantise_x()
         natural_add(0, 6, nc.vector)
         interleave(0, 6)
+        round_out(5)
         finish_nope(1, True)
         finish_nope(0, False)
         finish_rope(0, 0, True)
         finish_rope(1, 0, False)
-        finish_rope(1, 1, True)
-        finish_rope(0, 1, False)
+        finish_rope(0, 1, True)
+        finish_rope(1, 1, False)

@@ -79,11 +79,11 @@ def tile_gptossmlaattention_pb_s_kernel(tc, hidden_states, cos, sin, Wq, bq, gra
         load_grad(1, 6, 1)
         load_table(1, SIN)
         load_grad(0, 2, 2)
-        load_grad(1, 7, 1)
         load_grad(1, 0, 1)
         load_grad(1, 1, 1)
-        load_grad(1, 2, 2)
+        load_grad(1, 7, 1)
         load_grad(0, 4, 2)
+        load_grad(1, 2, 2)
         nc.sync.dma_start(out=x_sb[:], in_=hidden_states[0].rearrange("(c p j) m -> p c j m", p=P, j=PACK))
         load_grad(1, 4, 2)
         load_grad(0, 6, 2)
@@ -208,20 +208,24 @@ def tile_gptossmlaattention_pb_s_kernel(tc, hidden_states, cos, sin, Wq, bq, gra
             engine, tables = worker
             by_sin = keep.tile([P, 2, PACK, ROPE], F32, name="by_sin_%d_%d" % (c, first))
             natural[c, first, SIN] = by_sin
-            lower, upper = slice(0, HALF), slice(HALF, ROPE)
-            for src, dst in ((upper, lower), (lower, upper)):
-                engine.tensor_tensor(
-                    out=by_sin[:, :, :, dst],
-                    in0=groups[c, first][:, :, :, NOPE:][:, :, :, src],
-                    in1=tables[c][:, SIN, :, src].unsqueeze(1).to_broadcast([P, 2, PACK, HALF]),
-                    op=MULT,
-                )
+            engine.tensor_tensor(
+                out=by_sin[:],
+                in0=groups[c, first][:, :, :, NOPE:],
+                in1=tables[c][:, SIN].unsqueeze(1).to_broadcast([P, 2, PACK, ROPE]),
+                op=MULT,
+            )
+
+        def halves(tile_ap):
+            return tile_ap.rearrange("p h j (u k) -> p (h j) u k", u=2)
 
         def natural_add(c, first, engine=nc.gpsimd):
             summed = keep.tile([P, 2, PACK, ROPE], BF16, name="summed_%d_%d" % (c, first))
             natural[c, first, "sum"] = summed
             engine.tensor_tensor(
-                out=summed[:], in0=natural[c, first, COS][:], in1=natural[c, first, SIN][:], op=ADD
+                out=halves(summed[:]),
+                in0=halves(natural[c, first, COS][:]),
+                in1=halves(natural[c, first, SIN][:])[:, :, ::-1, :],
+                op=ADD,
             )
 
         def interleave(c, first):
@@ -292,30 +296,30 @@ def tile_gptossmlaattention_pb_s_kernel(tc, hidden_states, cos, sin, Wq, bq, gra
         natural_cos(on_vector_from_sbuf, 0, 0, 1, 1)
         regroup_nope(0, 1, 1)
         natural_cos(on_gpsimd, 1, 6, 0, 1)
+        regroup_nope(1, 6, 1)
         negate_lower_sin(1)
         flipped = rt_pool.tile([P, 2, PACK, P], BF16, name="rt")
         for t in (COS, SIN):
             for j in range(PACK):
                 nc.tensor.transpose(flipped[:, t, j, :], table_sb[1][:, t, j, :], ident_bf[:])
         natural_sin(on_vector, 0, 0)
+        natural_add(0, 0)
         natural_cos(on_gpsimd, 1, 6, 1, 1)
         transpose_r(0)
         nc.scalar.copy(out=table_t[:], in_=flipped[:])
         transpose_r(1)
-        natural_add(0, 0)
         natural_cos(on_vector, 0, 2)
-        regroup_nope(1, 6, 1)
         regroup_nope(0, 2, 2)
-        regroup_nope(1, 7, 1)
         regroup_nope(1, 0, 1)
         regroup_nope(1, 1, 1)
+        regroup_nope(1, 7, 1)
         natural_sin(on_vector, 0, 2)
         natural_sin(on_gpsimd, 1, 6)
-        regroup_nope(1, 2, 2)
-        regroup_nope(0, 4, 2)
         unit(0)
-        natural_cos(on_vector, 0, 4)
         interleave(0, 0)
+        regroup_nope(0, 4, 2)
+        natural_cos(on_vector, 0, 4)
+        regroup_nope(1, 2, 2)
         regroup_x()
         round_out(0)
         regroup_nope(1, 4, 2)

@@ -77,8 +77,9 @@ def tile_gptossmlaattention_pb_s_kernel(tc, hidden_states, cos, sin, Wq, bq, gra
         load_grad(0, 1, 1)
         load_table(1, COS)
         load_grad(1, 6, 1)
+        load_grad(0, 2, 1)
         load_table(1, SIN)
-        load_grad(0, 2, 2)
+        load_grad(0, 3, 1)
         load_grad(1, 0, 1)
         load_grad(1, 1, 1)
         load_grad(1, 7, 1)
@@ -192,26 +193,27 @@ def tile_gptossmlaattention_pb_s_kernel(tc, hidden_states, cos, sin, Wq, bq, gra
         on_vector_from_sbuf = (nc.vector, table_sb)
         on_gpsimd = (nc.gpsimd, table_sb)
 
-        def natural_cos(worker, c, first, place=0, count=2):
+        def products_of(c, first):
+            if (c, first) not in natural:
+                both = keep.tile([P, 2, 2, PACK, ROPE], F32, name="natural_%d_%d" % (c, first))
+                natural[c, first] = both
+            return natural[c, first]
+
+        def natural_one(worker, t, c, first, place=0, count=2):
             engine, tables = worker
-            if (c, first, COS) not in natural:
-                by_cos = keep.tile([P, 2, PACK, ROPE], F32, name="by_cos_%d_%d" % (c, first))
-                natural[c, first, COS] = by_cos
             engine.tensor_tensor(
-                out=natural[c, first, COS][:, place : place + count],
+                out=products_of(c, first)[:, t, place : place + count],
                 in0=groups[c, first][:, place : place + count, :, NOPE:],
-                in1=tables[c][:, COS].unsqueeze(1).to_broadcast([P, count, PACK, ROPE]),
+                in1=tables[c][:, t].unsqueeze(1).to_broadcast([P, count, PACK, ROPE]),
                 op=MULT,
             )
 
-        def natural_sin(worker, c, first):
-            engine, tables = worker
-            by_sin = keep.tile([P, 2, PACK, ROPE], F32, name="by_sin_%d_%d" % (c, first))
-            natural[c, first, SIN] = by_sin
-            engine.tensor_tensor(
-                out=by_sin[:],
-                in0=groups[c, first][:, :, :, NOPE:],
-                in1=tables[c][:, SIN].unsqueeze(1).to_broadcast([P, 2, PACK, ROPE]),
+        def natural_head(c, head):
+            first = group_of[c, head]
+            nc.vector.tensor_tensor(
+                out=products_of(c, first)[:, :, head - first],
+                in0=grad[c, head][:, :, NOPE:].unsqueeze(1).to_broadcast([P, 2, PACK, ROPE]),
+                in1=table_ps[:],
                 op=MULT,
             )
 
@@ -223,8 +225,8 @@ def tile_gptossmlaattention_pb_s_kernel(tc, hidden_states, cos, sin, Wq, bq, gra
             natural[c, first, "sum"] = summed
             engine.tensor_tensor(
                 out=halves(summed[:]),
-                in0=halves(natural[c, first, COS][:]),
-                in1=halves(natural[c, first, SIN][:])[:, :, ::-1, :],
+                in0=halves(natural[c, first][:, COS]),
+                in1=halves(natural[c, first][:, SIN])[:, :, ::-1, :],
                 op=ADD,
             )
 
@@ -239,7 +241,7 @@ def tile_gptossmlaattention_pb_s_kernel(tc, hidden_states, cos, sin, Wq, bq, gra
         acc_nope = fixed.tile([P, N_TILE], F32, name="acc_nope")
         acc_rope = [fixed.tile([P, N_TILE], F32, name="acc_rope_%d" % n) for n in range(HEADS // TILE_HEADS)]
 
-        def quantise_and_multiply(c, grouped, acc, out_columns, name, first_pass):
+        def quantise_and_multiply(c, grouped, acc, out_columns, name, first_pass, last=False):
             codes = keep.tile([P, N_TILE], U32, name="codes_" + name, align_bytes=64)
             scales = keep.tile([P, N_TILE], U8, name="scales_" + name, align_bytes=64)
             nc.vector.quantize_mx(out=codes[:].bitcast(E5M2_X4), scales=scales[:], in_=grouped)
@@ -254,12 +256,17 @@ def tile_gptossmlaattention_pb_s_kernel(tc, hidden_states, cos, sin, Wq, bq, gra
             )
             if not first_pass:
                 result = keep.tile([P, N_TILE], F32, name="result_" + name)
-                nc.scalar.copy(out=result[:], in_=acc[:])
-                nc.sync.dma_start(
-                    out=out_columns, in_=result[:].rearrange("m (h d) -> m h d", h=out_columns.shape[1])
-                )
+                heads = out_columns.shape[1]
+                pieces = 2 if last else 1
+                for piece, queue in zip(range(pieces), (nc.sync, nc.scalar)):
+                    columns = slice(piece * N_TILE // pieces, (piece + 1) * N_TILE // pieces)
+                    nc.scalar.copy(out=result[:, columns], in_=acc[:, columns])
+                    queue.dma_start(
+                        out=out_columns[:, piece * heads // pieces : (piece + 1) * heads // pieces],
+                        in_=result[:, columns].rearrange("m (h d) -> m h d", h=heads // pieces),
+                    )
 
-        def finish_rope(c, n, first_pass):
+        def finish_rope(c, n, first_pass, last=False):
             quantise_and_multiply(
                 c,
                 rope_grouped[c, n][:].rearrange("p h i j -> p (h i j)"),
@@ -267,6 +274,7 @@ def tile_gptossmlaattention_pb_s_kernel(tc, hidden_states, cos, sin, Wq, bq, gra
                 out_heads[:, n * TILE_HEADS : (n + 1) * TILE_HEADS, NOPE:],
                 "rope_%d_%d" % (c, n),
                 first_pass,
+                last,
             )
 
         def finish_nope(c, first_pass):
@@ -290,35 +298,36 @@ def tile_gptossmlaattention_pb_s_kernel(tc, hidden_states, cos, sin, Wq, bq, gra
                 transpose_r(h + 2)
 
         copy_table_to_psum(COS)
-        natural_cos(on_vector_from_sbuf, 0, 0, 0, 1)
+        natural_one(on_vector_from_sbuf, COS, 0, 0, 0, 1)
         copy_table_to_psum(SIN)
         regroup_nope(0, 0, 1)
-        natural_cos(on_vector_from_sbuf, 0, 0, 1, 1)
+        natural_one(on_vector_from_sbuf, COS, 0, 0, 1, 1)
         regroup_nope(0, 1, 1)
-        natural_cos(on_gpsimd, 1, 6, 0, 1)
+        natural_one(on_gpsimd, COS, 1, 6, 0, 1)
         regroup_nope(1, 6, 1)
+        regroup_nope(0, 2, 1)
         negate_lower_sin(1)
         flipped = rt_pool.tile([P, 2, PACK, P], BF16, name="rt")
         for t in (COS, SIN):
             for j in range(PACK):
                 nc.tensor.transpose(flipped[:, t, j, :], table_sb[1][:, t, j, :], ident_bf[:])
-        natural_sin(on_vector, 0, 0)
+        natural_one(on_vector, SIN, 0, 0)
         natural_add(0, 0)
-        natural_cos(on_gpsimd, 1, 6, 1, 1)
+        natural_one(on_gpsimd, COS, 1, 6, 1, 1)
         transpose_r(0)
         nc.scalar.copy(out=table_t[:], in_=flipped[:])
         transpose_r(1)
-        natural_cos(on_vector, 0, 2)
-        regroup_nope(0, 2, 2)
+        natural_head(0, 2)
+        regroup_nope(0, 3, 1)
         regroup_nope(1, 0, 1)
         regroup_nope(1, 1, 1)
         regroup_nope(1, 7, 1)
-        natural_sin(on_vector, 0, 2)
-        natural_sin(on_gpsimd, 1, 6)
+        natural_head(0, 3)
+        natural_one(on_gpsimd, SIN, 1, 6)
         unit(0)
         interleave(0, 0)
         regroup_nope(0, 4, 2)
-        natural_cos(on_vector, 0, 4)
+        natural_head(0, 4)
         regroup_nope(1, 2, 2)
         regroup_x()
         round_out(0)
@@ -326,14 +335,14 @@ def tile_gptossmlaattention_pb_s_kernel(tc, hidden_states, cos, sin, Wq, bq, gra
         unit(1)
         regroup_nope(0, 6, 2)
         round_out(1)
-        natural_sin(on_vector, 0, 4)
+        natural_head(0, 5)
         natural_add(0, 2)
         unit(2)
         interleave(0, 2)
         round_out(2)
-        natural_cos(on_vector, 0, 6)
+        natural_head(0, 6)
         unit(3)
-        natural_sin(on_vector, 0, 6)
+        natural_head(0, 7)
         natural_add(1, 6)
         natural_add(0, 4)
         interleave(1, 6)
@@ -351,4 +360,4 @@ def tile_gptossmlaattention_pb_s_kernel(tc, hidden_states, cos, sin, Wq, bq, gra
         finish_rope(0, 0, True)
         finish_rope(1, 0, False)
         finish_rope(0, 1, True)
-        finish_rope(1, 1, False)
+        finish_rope(1, 1, False, True)

@@ -27,6 +27,7 @@ N_TILE = 512
 TILE_HEADS = N_TILE // ROPE
 COS, SIN = 0, 1
 ROAD_HEADS = 6
+RUN = 4
 
 FLOPS = 2 * HID * HEADS * HEAD * TOKENS
 BYTES = 2 * (TOKENS * HID + 2 * TOKENS * ROPE + HEADS * TOKENS * HEAD) + 4 * HID * HEADS * HEAD
@@ -127,7 +128,10 @@ def tile_gptossmlaattention_pb_s_kernel(tc, hidden_states, cos, sin, Wq, bq, gra
         x_scales = keep.tile([P, PASSES, HID], U8, name="x_scales", align_bytes=64)
 
         def regroup_x():
-            nc.scalar.copy(out=x_grouped[:], in_=x_sb[:].rearrange("p c j m -> p c m j"))
+            nc.scalar.copy(
+                out=x_grouped[:].rearrange("p c (g i) j -> p c g j i", i=RUN),
+                in_=x_sb[:].rearrange("p c j (g i) -> p c g j i", i=RUN),
+            )
 
         def quantise_x():
             nc.vector.quantize_mx(
@@ -148,8 +152,10 @@ def tile_gptossmlaattention_pb_s_kernel(tc, hidden_states, cos, sin, Wq, bq, gra
         def regroup_nope(c, head, count):
             place = head - group_of[c, head]
             nc.scalar.copy(
-                out=nope_grouped[c][:, head : head + count],
-                in_=groups[c, group_of[c, head]][:, place : place + count, :, :NOPE].rearrange("p h j d -> p h d j"),
+                out=nope_grouped[c][:, head : head + count].rearrange("p h (g i) j -> p h g j i", i=RUN),
+                in_=groups[c, group_of[c, head]][:, place : place + count, :, :NOPE].rearrange(
+                    "p h j (g i) -> p h g j i", i=RUN
+                ),
             )
 
         r_t = {}
@@ -233,8 +239,10 @@ def tile_gptossmlaattention_pb_s_kernel(tc, hidden_states, cos, sin, Wq, bq, gra
         def interleave(c, first):
             place = first % TILE_HEADS
             nc.scalar.copy(
-                out=rope_grouped[c, first // TILE_HEADS][:, place : place + 2],
-                in_=natural[c, first, "sum"][:].rearrange("p h j i -> p h i j"),
+                out=rope_grouped[c, first // TILE_HEADS][:, place : place + 2].rearrange(
+                    "p h (g i) j -> p h g j i", i=RUN
+                ),
+                in_=natural[c, first, "sum"][:].rearrange("p h j (g i) -> p h g j i", i=RUN),
             )
 
         out_heads = out.rearrange("m (h d) -> m h d", d=HEAD)

from contextlib import ExitStack

import concourse.mybir as mybir
from concourse.masks import make_identity

BF16 = mybir.dt.bfloat16
F32 = mybir.dt.float32
U32 = mybir.dt.uint32
U8 = mybir.dt.uint8
E4M3_X4 = mybir.dt.float8_e4m3fn_x4
E5M2_X4 = mybir.dt.float8_e5m2_x4
MULT = mybir.AluOpType.mult
ADD = mybir.AluOpType.add

P = 128
PACK = 4
K_PASS = P * PACK
TOKENS = 1024
PASSES = TOKENS // K_PASS
HID = 128
HEADS = 8
NOPE = 64
ROPE = 128
HALF = ROPE // 2
HEAD = NOPE + ROPE
N_TILE = 512
TILE_HEADS = N_TILE // ROPE
COS, SIN = 0, 1
ROAD_HEADS = 6
RUN = 4

FLOPS = 2 * HID * HEADS * HEAD * TOKENS
BYTES = 2 * (TOKENS * HID + 2 * TOKENS * ROPE + HEADS * TOKENS * HEAD) + 4 * HID * HEADS * HEAD


def tile_gptossmlaattention_pb_s_kernel(tc, hidden_states, cos, sin, Wq, bq, grad_out, out):
    nc = tc.nc
    with ExitStack() as ctx:
        ctx.enter_context(tc.manual_schedule())
        keep = ctx.enter_context(tc.tile_pool(name="keep", bufs=1))
        fixed = ctx.enter_context(tc.psum_pool(name="fixed", bufs=1))
        rt_pool = ctx.enter_context(tc.psum_pool(name="rt", bufs=2))
        sum_pool = ctx.enter_context(tc.psum_pool(name="sum", bufs=2))

        table_sb = [keep.tile([P, 2, PACK, ROPE], BF16, name="table_sb_%d" % c) for c in range(PASSES)]

        def load_table(c, t):
            nc.sync.dma_start(
                out=table_sb[c][:, t],
                in_=(cos, sin)[t][0, c * K_PASS : (c + 1) * K_PASS, :].rearrange("(p j) i -> p j i", j=PACK),
            )

        grad = {}
        groups = {}
        group_of = {}
        for c, first, count in (
            (0, 0, 2), (0, 2, 2), (0, 4, 2), (0, 6, 2), (1, 0, 1), (1, 1, 1), (1, 2, 2), (1, 4, 2), (1, 6, 2)
        ):
            group = keep.tile([P, count, PACK, HEAD], BF16, name="grad_%d_%d" % (c, first))
            groups[c, first] = group
            for h in range(count):
                grad[c, first + h] = group[:, h]
                group_of[c, first + h] = first

        def load_grad(c, head, count):
            place = head - group_of[c, head]
            nc.sync.dma_start(
                out=groups[c, group_of[c, head]][:, place : place + count],
                in_=grad_out[0, head : head + count, c * K_PASS : (c + 1) * K_PASS, :].rearrange(
                    "h (p j) d -> p h j d", j=PACK
                ),
            )

        x_sb = keep.tile([P, PASSES, PACK, HID], BF16, name="x_sb")
        load_table(0, COS)
        load_grad(0, 0, 1)
        load_table(0, SIN)
        load_grad(0, 1, 1)
        load_table(1, COS)
        load_grad(1, 6, 1)
        load_grad(0, 2, 1)
        load_table(1, SIN)
        load_grad(0, 3, 1)
        load_grad(1, 0, 1)
        load_grad(1, 1, 1)
        load_grad(1, 7, 1)
        load_grad(0, 4, 2)
        load_grad(1, 2, 2)
        nc.sync.dma_start(out=x_sb[:], in_=hidden_states[0].rearrange("(c p j) m -> p c j m", p=P, j=PACK))
        load_grad(1, 4, 2)
        load_grad(0, 6, 2)

        ident_bf = keep.tile([P, P], BF16, name="ident_bf")
        make_identity(nc, ident_bf[:])
        ident_f = keep.tile([P, P], F32, name="ident_f")
        swap_f = keep.tile([P, P], F32, name="swap_f")
        minus_ident_bf = keep.tile([P, P], BF16, name="minus_ident_bf")
        nc.vector.tensor_scalar_mul(out=minus_ident_bf[:], in0=ident_bf[:], scalar1=-1.0)
        nc.vector.tensor_copy(out=ident_f[:], in_=ident_bf[:])
        nc.vector.tensor_copy(out=swap_f[:, :HALF], in_=ident_bf[:, HALF:])
        nc.vector.tensor_copy(out=swap_f[:, HALF:], in_=ident_bf[:, :HALF])

        table_ps = fixed.tile([P, 2, PACK, ROPE], BF16, name="table_ps")

        def copy_table_to_psum(t):
            if t == COS:
                nc.tensor.matmul(
                    out=table_ps[:, t].rearrange("p j i -> p (j i)"),
                    lhsT=ident_bf[:],
                    rhs=table_sb[0][:, t].rearrange("p j i -> p (j i)"),
                    start=True,
                    stop=True,
                )
            else:
                for half, matrix in ((slice(0, HALF), minus_ident_bf), (slice(HALF, ROPE), ident_bf)):
                    nc.tensor.matmul(
                        out=table_ps[:, t, :, half],
                        lhsT=matrix[:],
                        rhs=table_sb[0][:, t, :, half],
                        start=True,
                        stop=True,
                    )

        table_t = keep.tile([P, 2, PACK, P], BF16, name="table_t")

        x_grouped = keep.tile([P, PASSES, HID, PACK], BF16, name="x_grouped", align_bytes=64)
        x_codes = keep.tile([P, PASSES, HID], U32, name="x_codes", align_bytes=64)
        x_scales = keep.tile([P, PASSES, HID], U8, name="x_scales", align_bytes=64)

        def regroup_x():
            nc.scalar.copy(
                out=x_grouped[:].rearrange("p c (g i) j -> p c g j i", i=RUN),
                in_=x_sb[:].rearrange("p c j (g i) -> p c g j i", i=RUN),
            )

        def quantise_x():
            nc.vector.quantize_mx(
                out=x_codes[:].rearrange("p c m -> p (c m)").bitcast(E4M3_X4),
                scales=x_scales[:].rearrange("p c m -> p (c m)"),
                in_=x_grouped[:].rearrange("p c m j -> p (c m j)"),
            )

        nope_grouped = [
            keep.tile([P, HEADS, NOPE, PACK], BF16, name="nope_grouped_%d" % c, align_bytes=64) for c in range(PASSES)
        ]
        rope_grouped = {
            (c, n): keep.tile([P, TILE_HEADS, ROPE, PACK], BF16, name="rope_grouped_%d_%d" % (c, n), align_bytes=64)
            for c in range(PASSES)
            for n in range(HEADS // TILE_HEADS)
        }

        def regroup_nope(c, head, count):
            place = head - group_of[c, head]
            nc.scalar.copy(
                out=nope_grouped[c][:, head : head + count].rearrange("p h (g i) j -> p h g j i", i=RUN),
                in_=groups[c, group_of[c, head]][:, place : place + count, :, :NOPE].rearrange(
                    "p h j (g i) -> p h g j i", i=RUN
                ),
            )

        r_t = {}
        prod_t = {}
        sums = {}

        def transpose_r(h):
            r_t[h] = rt_pool.tile([P, PACK, P], BF16, name="rt")
            for j in range(PACK):
                nc.tensor.transpose(r_t[h][:, j, :], grad[1, h][:, j, NOPE:], ident_bf[:])

        def products(h):
            prod_t[h] = keep.tile([P, 2, PACK, P], F32, name="prod_t_%d" % h)
            nc.vector.tensor_tensor(
                out=prod_t[h][:],
                in0=table_t[:],
                in1=r_t[h][:].unsqueeze(1).to_broadcast([P, 2, PACK, P]),
                op=MULT,
            )

        def add_up(h):
            sums[h] = sum_pool.tile([P, PACK, ROPE], F32, name="sum")
            for j in range(PACK):
                nc.tensor.matmul(
                    out=sums[h][:, j, :], lhsT=prod_t[h][:, COS, j, :], rhs=ident_f[:],
                    is_transpose=True, start=True, stop=False,
                )
                nc.tensor.matmul(
                    out=sums[h][:, j, :], lhsT=prod_t[h][:, SIN, j, :], rhs=swap_f[:],
                    is_transpose=True, start=False, stop=True,
                )

        def round_out(h):
            nc.scalar.copy(
                out=rope_grouped[1, h // TILE_HEADS][:, h % TILE_HEADS],
                in_=sums[h][:].rearrange("p j i -> p i j"),
            )

        natural = {}
        on_vector = (nc.vector, (table_ps, None))
        on_vector_from_sbuf = (nc.vector, table_sb)
        on_gpsimd = (nc.gpsimd, table_sb)

        def products_of(c, first):
            if (c, first) not in natural:
                both = keep.tile([P, 2, 2, PACK, ROPE], F32, name="natural_%d_%d" % (c, first))
                natural[c, first] = both
            return natural[c, first]

        def natural_one(worker, t, c, first, place=0, count=2):
            engine, tables = worker
            engine.tensor_tensor(
                out=products_of(c, first)[:, t, place : place + count],
                in0=groups[c, first][:, place : place + count, :, NOPE:],
                in1=tables[c][:, t].unsqueeze(1).to_broadcast([P, count, PACK, ROPE]),
                op=MULT,
            )

        def natural_head(c, head):
            first = group_of[c, head]
            nc.vector.tensor_tensor(
                out=products_of(c, first)[:, :, head - first],
                in0=grad[c, head][:, :, NOPE:].unsqueeze(1).to_broadcast([P, 2, PACK, ROPE]),
                in1=table_ps[:],
                op=MULT,
            )

        def halves(tile_ap):
            return tile_ap.rearrange("p h j (u k) -> p (h j) u k", u=2)

        def natural_add(c, first, engine=nc.gpsimd):
            summed = keep.tile([P, 2, PACK, ROPE], BF16, name="summed_%d_%d" % (c, first))
            natural[c, first, "sum"] = summed
            engine.tensor_tensor(
                out=halves(summed[:]),
                in0=halves(natural[c, first][:, COS]),
                in1=halves(natural[c, first][:, SIN])[:, :, ::-1, :],
                op=ADD,
            )

        def interleave(c, first):
            place = first % TILE_HEADS
            nc.scalar.copy(
                out=rope_grouped[c, first // TILE_HEADS][:, place : place + 2].rearrange(
                    "p h (g i) j -> p h g j i", i=RUN
                ),
                in_=natural[c, first, "sum"][:].rearrange("p h j (g i) -> p h g j i", i=RUN),
            )

        out_heads = out.rearrange("m (h d) -> m h d", d=HEAD)
        acc_nope = fixed.tile([P, N_TILE], F32, name="acc_nope")
        acc_rope = [fixed.tile([P, N_TILE], F32, name="acc_rope_%d" % n) for n in range(HEADS // TILE_HEADS)]

        def quantise_and_multiply(c, grouped, acc, out_columns, name, first_pass, last=False):
            codes = keep.tile([P, N_TILE], U32, name="codes_" + name, align_bytes=64)
            scales = keep.tile([P, N_TILE], U8, name="scales_" + name, align_bytes=64)
            nc.vector.quantize_mx(out=codes[:].bitcast(E5M2_X4), scales=scales[:], in_=grouped)
            nc.tensor.matmul_mx(
                out=acc[:],
                lhsT=x_codes[:, c, :].bitcast(E4M3_X4),
                lhsT_scale=x_scales[:, c, :],
                rhs=codes[:].bitcast(E5M2_X4),
                rhs_scale=scales[:],
                start=first_pass,
                stop=not first_pass,
            )
            if not first_pass:
                result = keep.tile([P, N_TILE], F32, name="result_" + name)
                heads = out_columns.shape[1]
                pieces = 2 if last else 1
                for piece, queue in zip(range(pieces), (nc.sync, nc.scalar)):
                    columns = slice(piece * N_TILE // pieces, (piece + 1) * N_TILE // pieces)
                    nc.scalar.copy(out=result[:, columns], in_=acc[:, columns])
                    queue.dma_start(
                        out=out_columns[:, piece * heads // pieces : (piece + 1) * heads // pieces],
                        in_=result[:, columns].rearrange("m (h d) -> m h d", h=heads // pieces),
                    )

        def finish_rope(c, n, first_pass, last=False):
            quantise_and_multiply(
                c,
                rope_grouped[c, n][:].rearrange("p h i j -> p (h i j)"),
                acc_rope[n],
                out_heads[:, n * TILE_HEADS : (n + 1) * TILE_HEADS, NOPE:],
                "rope_%d_%d" % (c, n),
                first_pass,
                last,
            )

        def finish_nope(c, first_pass):
            quantise_and_multiply(
                c,
                nope_grouped[c][:].rearrange("p h d j -> p (h d j)"),
                acc_nope,
                out_heads[:, :, :NOPE],
                "nope_%d" % c,
                first_pass,
            )

        def negate_lower_sin(c):
            lower_sin = table_sb[c][:, SIN, :, :HALF]
            nc.scalar.mul(out=lower_sin, in_=lower_sin, mul=-1.0)

        def unit(h):
            products(h)
            add_up(h)
            if h + 2 < ROAD_HEADS:
                transpose_r(h + 2)

        copy_table_to_psum(COS)
        natural_one(on_vector_from_sbuf, COS, 0, 0, 0, 1)
        copy_table_to_psum(SIN)
        regroup_nope(0, 0, 1)
        natural_one(on_vector_from_sbuf, COS, 0, 0, 1, 1)
        regroup_nope(0, 1, 1)
        natural_one(on_gpsimd, COS, 1, 6, 0, 1)
        regroup_nope(1, 6, 1)
        regroup_nope(0, 2, 1)
        negate_lower_sin(1)
        flipped = rt_pool.tile([P, 2, PACK, P], BF16, name="rt")
        for t in (COS, SIN):
            for j in range(PACK):
                nc.tensor.transpose(flipped[:, t, j, :], table_sb[1][:, t, j, :], ident_bf[:])
        natural_one(on_vector, SIN, 0, 0)
        natural_add(0, 0)
        natural_one(on_gpsimd, COS, 1, 6, 1, 1)
        transpose_r(0)
        nc.scalar.copy(out=table_t[:], in_=flipped[:])
        transpose_r(1)
        natural_head(0, 2)
        regroup_nope(0, 3, 1)
        regroup_nope(1, 0, 1)
        regroup_nope(1, 1, 1)
        regroup_nope(1, 7, 1)
        natural_head(0, 3)
        natural_one(on_gpsimd, SIN, 1, 6)
        unit(0)
        interleave(0, 0)
        regroup_nope(0, 4, 2)
        natural_head(0, 4)
        regroup_nope(1, 2, 2)
        regroup_x()
        round_out(0)
        regroup_nope(1, 4, 2)
        unit(1)
        regroup_nope(0, 6, 2)
        round_out(1)
        natural_head(0, 5)
        natural_add(0, 2)
        unit(2)
        interleave(0, 2)
        round_out(2)
        natural_head(0, 6)
        unit(3)
        natural_head(0, 7)
        natural_add(1, 6)
        natural_add(0, 4)
        interleave(1, 6)
        round_out(3)
        unit(4)
        unit(5)
        interleave(0, 4)
        round_out(4)
        quantise_x()
        natural_add(0, 6, nc.vector)
        interleave(0, 6)
        round_out(5)
        finish_nope(1, True)
        finish_nope(0, False)
        finish_rope(0, 0, True)
        finish_rope(1, 0, False)
        finish_rope(0, 1, True)
        finish_rope(1, 1, False, True)
